import numpy as np
import ml_dtypes


def mxq(x, axis, fmt="e4m3"):
    dtype, down = {"e4m3": (ml_dtypes.float8_e4m3fn, 7), "e5m2": (ml_dtypes.float8_e5m2, 14)}[fmt]
    v = np.moveaxis(np.asarray(x, np.float32).astype(ml_dtypes.bfloat16).astype(np.float64), axis, -1)
    blocks = v.reshape(v.shape[:-1] + (-1, 32))
    amax = np.abs(blocks).max(-1, keepdims=True)
    byte = np.maximum(np.where(amax > 0, np.frexp(amax)[1] - 1 + 127, 0) - down, 1)
    scale = np.exp2(byte - 127.0)
    codes = (blocks / scale).astype(np.float32).astype(dtype).astype(np.float64)
    return np.moveaxis((codes * scale).reshape(v.shape), -1, axis)


WIDE = False


def mx_kscale(k):
    if not WIDE:
        return np.ones(k)
    levels = np.array([10, -10, 5, -5, 0])
    a = np.random.permutation(np.resize(levels, k // 512 * 4)).reshape(k // 512, 4)
    idx = np.arange(k)
    return np.exp2(a[idx // 512, idx % 128 // 32])


BF16 = ml_dtypes.bfloat16


def bf(x):
    return np.asarray(x, np.float32).astype(BF16)


def f64(x):
    return np.asarray(x).astype(np.float64)


N, D = 1024, 512
EPS = 1e-5


def setup_inputs():
    s, t = mx_kscale(D), mx_kscale(D)
    k_off = np.random.standard_normal(D)
    return {"q": bf(np.random.standard_normal((N, D)) * 0.7 * s),
            "k": bf((np.random.standard_normal((N, D)) + k_off) * 0.5 / s),
            "x": bf(np.random.standard_normal((N, D)) * t),
            "Wv": bf(np.random.standard_normal((D, D)) * 4.0 / np.sqrt(D) / t),
            "bv": bf(np.random.standard_normal(D) * 0.05)}


def reference(q, k, x, Wv, bv):
    cc = np.sqrt(D)
    v = (mxq(f64(x), 1, "e4m3") @ mxq(f64(Wv), 1, "e4m3").T) + f64(bv)
    s = mxq(f64(q), 1, "e4m3") @ mxq(f64(k), 1, "e4m3").T
    mean = s.mean(-1, keepdims=True)
    var = s.var(-1, keepdims=True, ddof=1)
    u = np.sin((s - mean) / np.sqrt(var + EPS)) / cc
    e = np.exp(u - u.max(-1, keepdims=True))
    return (mxq(e, 1, "e4m3") @ mxq(v, 0, "e4m3")) / e.sum(-1, keepdims=True)

@@ -1,0 +1,306 @@
+import math
+from contextlib import ExitStack
+
+import concourse.mybir as mybir
+from concourse.masks import make_identity
+
+F32 = mybir.dt.float32
+BF16 = mybir.dt.bfloat16
+U32 = mybir.dt.uint32
+U8 = mybir.dt.uint8
+FP8X4 = mybir.dt.float8_e4m3fn_x4
+ALU = mybir.AluOpType
+ACT = mybir.ActivationFunctionType
+AXIS = mybir.AxisListType
+
+P = 128
+PACK = 4
+ROWS = 1024
+FEATURES = 512
+ROW_TILES = ROWS // P
+KEY_PASSES = ROWS // (P * PACK)
+EPS = 1e-5
+FLOPS = 2 * ROWS * FEATURES * FEATURES + 2 * 2 * ROWS * ROWS * FEATURES
+
+TWO_PI = 2.0 * math.pi
+INV_SQRT_FEATURES = 1.0 / math.sqrt(FEATURES)
+ROUND_MAGIC = 12582912.0
+
+
+def tile_selfattentionlayer_pa_kernel(tc, q, k, x, Wv, bv, out):
+    nc = tc.nc
+    with ExitStack() as ctx:
+        const = ctx.enter_context(tc.tile_pool(name="const", bufs=1))
+        inputs = ctx.enter_context(tc.tile_pool(name="inputs", bufs=1))
+        operands = ctx.enter_context(tc.tile_pool(name="operands", bufs=1))
+        grouped_pool = ctx.enter_context(tc.tile_pool(name="grouped", bufs=4))
+        angle_pool = ctx.enter_context(tc.tile_pool(name="angle", bufs=3))
+        small = ctx.enter_context(tc.tile_pool(name="small", bufs=8))
+        e_pool = ctx.enter_context(tc.tile_pool(name="e", bufs=3))
+        out_pool = ctx.enter_context(tc.tile_pool(name="out", bufs=3))
+        tr_banks = ctx.enter_context(tc.psum_pool(name="tr_banks", bufs=2))
+        acc_banks = ctx.enter_context(tc.psum_pool(name="acc_banks", bufs=6))
+        ctx.enter_context(tc.manual_schedule())
+
+        ident = const.tile([P, P], F32, name="ident")
+        make_identity(nc, ident[:])
+        ones = const.tile([P, P], BF16, name="ones")
+        nc.vector.memset(ones[:], 1.0)
+        bias_row = const.tile([P, FEATURES], BF16, name="bias_row")
+        nc.vector.memset(bias_row[:], 0.0)
+        neg_half = const.tile([P, 1], F32, name="neg_half")
+        nc.vector.memset(neg_half[:], -0.5)
+        warm = const.tile([P, 1], F32, name="warm")
+        nc.scalar.activation(out=warm[:], in_=neg_half[:], func=ACT.Sin)
+
+        nc.sync.dma_start(out=bias_row[0:1, :], in_=bv.rearrange("(o d) -> o d", o=1))
+        wv_sb = inputs.tile([P, 4, FEATURES], BF16, name="wv_sb")
+        nc.sync.dma_start(out=wv_sb[:], in_=Wv.rearrange("(t p) d -> p t d", p=P))
+        x_sb = inputs.tile([P, 4, 2, FEATURES], BF16, name="x_sb")
+        k_sb = inputs.tile([P, ROW_TILES, FEATURES], BF16, name="k_sb")
+        q_sb = inputs.tile([P, ROW_TILES, FEATURES], BF16, name="q_sb")
+        for c in range(4):
+            nc.sync.dma_start(
+                out=x_sb[:, c, :, :], in_=x[c * 256 : (c + 1) * 256, :].rearrange("(p e) d -> p e d", e=2)
+            )
+        for src, dst in ((k, k_sb), (q, q_sb)):
+            for c in range(4):
+                nc.sync.dma_start(
+                    out=dst[:, 2 * c : 2 * c + 2, :],
+                    in_=src[c * 256 : (c + 1) * 256, :].rearrange("(t p) d -> p t d", p=P),
+                )
+
+        def last_axis_to_partitions(block_a, block_b, grouped):
+            bank = tr_banks.tile([P, 2, 2, P], F32, tag="tr", name="tr_bank")
+            for b, block in enumerate((block_a, block_b)):
+                words = block.bitcast(F32)
+                for u in range(2):
+                    nc.tensor.transpose(
+                        out=bank[:, b, u, :], in_=words[:, u * P : (u + 1) * P], identity=ident[:]
+                    )
+            nc.scalar.copy(
+                out=grouped.bitcast(F32).rearrange("p (b r u) -> p b r u", b=2, u=2),
+                in_=bank[:].rearrange("p b u r -> p b r u"),
+            )
+
+        def new_grouped():
+            return grouped_pool.tile([P, 2 * P * PACK], BF16, align_bytes=64, tag="grouped", name="grouped")
+
+        def new_operand(columns, name):
+            codes = operands.tile([P, columns], U32, align_bytes=64, name=name + "_codes")
+            scales = operands.tile([P, columns], U8, align_bytes=64, name=name + "_scales")
+            return codes, scales
+
+        def quantise_rows(blocks, codes, scales):
+            for c in range(len(blocks) // 2):
+                grouped = new_grouped()
+                last_axis_to_partitions(blocks[2 * c], blocks[2 * c + 1], grouped[:])
+                cols = slice(c * 2 * P, (c + 1) * 2 * P)
+                nc.vector.quantize_mx(
+                    out=codes[:, cols].bitcast(FP8X4), scales=scales[:, cols], in_=grouped[:]
+                )
+
+        bias_bank = acc_banks.tile([P, FEATURES], F32, tag="acc", name="bias_bank")
+        nc.tensor.matmul(out=bias_bank[:], lhsT=ones[:], rhs=bias_row[:], start=True, stop=True)
+        bias_all = const.tile([P, FEATURES], F32, name="bias_all")
+        nc.scalar.copy(out=bias_all[:], in_=bias_bank[:])
+
+        wv_codes, wv_scales = new_operand(FEATURES, "wv")
+        x_codes, x_scales = new_operand(ROWS, "x")
+        k_codes, k_scales = new_operand(ROWS, "k")
+        q_codes, q_scales = new_operand(ROWS, "q")
+        v_grouped = operands.tile([P, KEY_PASSES, FEATURES, PACK], BF16, align_bytes=64, name="v_grouped")
+        v_codes = operands.tile([P, KEY_PASSES, FEATURES], U32, align_bytes=64, name="v_codes")
+        v_scales = operands.tile([P, KEY_PASSES, FEATURES], U8, align_bytes=64, name="v_scales")
+
+        def value_pass(g):
+            for c in range(FEATURES // P):
+                feats = slice(c * P, (c + 1) * P)
+                v_bank = acc_banks.tile([P, PACK, P], F32, tag="acc", name="v_bank")
+                for j in range(PACK):
+                    rows = slice((PACK * g + j) * P, (PACK * g + j + 1) * P)
+                    nc.tensor.matmul_mx(
+                        out=v_bank[:, j, :],
+                        lhsT=x_codes[:, rows].bitcast(FP8X4),
+                        lhsT_scale=x_scales[:, rows],
+                        rhs=wv_codes[:, feats].bitcast(FP8X4),
+                        rhs_scale=wv_scales[:, feats],
+                        start=True,
+                        stop=True,
+                    )
+                nc.vector.tensor_tensor(
+                    out=v_grouped[:, g, feats, :],
+                    in0=v_bank[:].rearrange("p j o -> p o j"),
+                    in1=bias_all[:, feats].unsqueeze(2).to_broadcast([P, P, PACK]),
+                    op=ALU.add,
+                )
+            nc.vector.quantize_mx(
+                out=v_codes[:, g, :].bitcast(FP8X4),
+                scales=v_scales[:, g, :],
+                in_=v_grouped[:, g, :, :].rearrange("p o j -> p (o j)"),
+            )
+
+        quantise_rows([wv_sb[:, t, :] for t in range(4)], wv_codes, wv_scales)
+        quantise_rows([x_sb[:, c, e, :] for c in range(4) for e in range(2)], x_codes, x_scales)
+        value_pass(0)
+        quantise_rows([k_sb[:, t, :] for t in range(ROW_TILES)], k_codes, k_scales)
+        quantise_rows([q_sb[:, t, :] for t in range(ROW_TILES)], q_codes, q_scales)
+        value_pass(1)
+
+        sines = operands.tile([P, ROW_TILES, ROWS], F32, name="sines")
+        s_banks, turn_scale, turn_bias, mean_var, turns, neg_frac = {}, {}, {}, {}, {}, {}
+
+        def scores(i):
+            queries = slice(i * P, (i + 1) * P)
+            s_banks[i] = [
+                acc_banks.tile([P, FEATURES], F32, tag="acc", name="s_bank%d" % h) for h in range(2)
+            ]
+            for h in range(2):
+                keys = slice(h * 512, (h + 1) * 512)
+                nc.tensor.matmul_mx(
+                    out=s_banks[i][h][:],
+                    lhsT=q_codes[:, queries].bitcast(FP8X4),
+                    lhsT_scale=q_scales[:, queries],
+                    rhs=k_codes[:, keys].bitcast(FP8X4),
+                    rhs_scale=k_scales[:, keys],
+                    start=True,
+                    stop=True,
+                )
+
+        def row_statistics(i):
+            stats = small.tile([P, 2, 6], F32, name="stats")
+            for h in range(2):
+                nc.vector.bn_stats(out=stats[:, h, :], in_=s_banks[i][h][:])
+            mean_var[i] = small.tile([P, 2], F32, name="mean_var")
+            nc.vector.bn_aggr(out=mean_var[i][:], in_=stats[:].rearrange("p h s -> p (h s)"))
+            scaled_var = small.tile([P, 1], F32, name="scaled_var")
+            nc.vector.tensor_scalar(
+                out=scaled_var[:],
+                in0=mean_var[i][:, 1:2],
+                scalar1=TWO_PI * TWO_PI * ROWS / (ROWS - 1),
+                scalar2=TWO_PI * TWO_PI * EPS,
+                op0=ALU.mult,
+                op1=ALU.add,
+            )
+            turn_scale[i] = small.tile([P, 1], F32, name="turn_scale")
+            nc.gpsimd.tensor_tensor(out=turn_scale[i][:], in0=scaled_var[:], in1=neg_half[:], op=ALU.pow)
+
+        def angle_in_turns(i):
+            turn_bias[i] = small.tile([P, 1], F32, name="turn_bias")
+            nc.vector.tensor_scalar(
+                out=turn_bias[i][:],
+                in0=mean_var[i][:, 0:1],
+                scalar1=turn_scale[i][:, 0:1],
+                scalar2=-1.0,
+                op0=ALU.mult,
+                op1=ALU.mult,
+            )
+            turns[i] = angle_pool.tile([P, ROWS], F32, name="turns")
+            for h in range(2):
+                nc.scalar.activation(
+                    out=turns[i][:, h * 512 : (h + 1) * 512],
+                    in_=s_banks[i][h][:],
+                    func=ACT.Identity,
+                    bias=turn_bias[i][:, 0:1],
+                    scale=turn_scale[i][:, 0:1],
+                )
+
+        def drop_whole_turns(i):
+            shifted = angle_pool.tile([P, ROWS], F32, name="shifted")
+            nc.vector.tensor_scalar(
+                out=shifted[:], in0=turns[i][:], scalar1=ROUND_MAGIC, scalar2=None, op0=ALU.add
+            )
+            neg_frac[i] = angle_pool.tile([P, ROWS], F32, name="neg_frac")
+            nc.vector.scalar_tensor_tensor(
+                out=neg_frac[i][:],
+                in0=shifted[:],
+                scalar=ROUND_MAGIC,
+                in1=turns[i][:],
+                op0=ALU.subtract,
+                op1=ALU.subtract,
+            )
+
+        def sine(i):
+            nc.scalar.activation(out=sines[:, i, :], in_=neg_frac[i][:], func=ACT.Sin, scale=-TWO_PI)
+
+        scores(0)
+        scores(1)
+        scores(2)
+        row_statistics(0)
+        for i in range(ROW_TILES):
+            if i + 1 < ROW_TILES:
+                row_statistics(i + 1)
+            angle_in_turns(i)
+            if i + 3 < ROW_TILES:
+                scores(i + 3)
+            if i >= 1:
+                drop_whole_turns(i - 1)
+                sine(i - 1)
+        drop_whole_turns(ROW_TILES - 1)
+        sine(ROW_TILES - 1)
+
+        exp_bias, row_sum, e_rows, e_grouped, out_banks, inv_sum = {}, {}, {}, {}, {}, {}
+
+        def row_maximum(i):
+            top = small.tile([P, 1], F32, name="top")
+            nc.vector.tensor_reduce(out=top[:], in_=sines[:, i, :], axis=AXIS.X, op=ALU.max)
+            exp_bias[i] = small.tile([P, 1], F32, name="exp_bias")
+            nc.vector.tensor_scalar(
+                out=exp_bias[i][:], in0=top[:], scalar1=-INV_SQRT_FEATURES, scalar2=None, op0=ALU.mult
+            )
+
+        def exponential(i):
+            e_rows[i] = e_pool.tile([P, ROWS], BF16, name="e_rows")
+            row_sum[i] = small.tile([P, 1], F32, name="row_sum")
+            nc.scalar.activation(
+                out=e_rows[i][:],
+                in_=sines[:, i, :],
+                func=ACT.Exp,
+                bias=exp_bias[i][:, 0:1],
+                scale=INV_SQRT_FEATURES,
+                accum_out=row_sum[i][:, 0:1],
+            )
+
+        def keys_to_partitions(i):
+            e_grouped[i] = new_grouped()
+            last_axis_to_partitions(e_rows[i][:, 0:512], e_rows[i][:, 512:1024], e_grouped[i][:])
+
+        def weighted_sum(i):
+            inv_sum[i] = small.tile([P, 1], F32, name="inv_sum")
+            nc.vector.reciprocal(out=inv_sum[i][:], in_=row_sum[i][:])
+            e_codes = e_pool.tile([P, KEY_PASSES * P], U32, align_bytes=64, name="e_codes")
+            e_scales = e_pool.tile([P, KEY_PASSES * P], U8, align_bytes=64, name="e_scales")
+            nc.vector.quantize_mx(out=e_codes[:].bitcast(FP8X4), scales=e_scales[:], in_=e_grouped[i][:])
+            out_banks[i] = acc_banks.tile([P, FEATURES], F32, tag="acc", name="out_bank")
+            for g in range(KEY_PASSES):
+                queries = slice(g * P, (g + 1) * P)
+                nc.tensor.matmul_mx(
+                    out=out_banks[i][:],
+                    lhsT=e_codes[:, queries].bitcast(FP8X4),
+                    lhsT_scale=e_scales[:, queries],
+                    rhs=v_codes[:, g, :].bitcast(FP8X4),
+                    rhs_scale=v_scales[:, g, :],
+                    start=(g == 0),
+                    stop=(g == KEY_PASSES - 1),
+                )
+
+        def divide_and_store(i):
+            result = out_pool.tile([P, FEATURES], F32, name="result")
+            nc.vector.tensor_scalar(
+                out=result[:], in0=out_banks[i][:], scalar1=inv_sum[i][:, 0:1], scalar2=None, op0=ALU.mult
+            )
+            nc.sync.dma_start(out=out[i * P : (i + 1) * P, :], in_=result[:])
+
+        row_maximum(0)
+        row_maximum(1)
+        for step in range(ROW_TILES + 3):
+            if step < ROW_TILES:
+                exponential(step)
+            if step + 2 < ROW_TILES:
+                row_maximum(step + 2)
+            if 0 <= step - 1 < ROW_TILES:
+                keys_to_partitions(step - 1)
+            if 0 <= step - 2 < ROW_TILES:
+                weighted_sum(step - 2)
+            if 0 <= step - 3 < ROW_TILES:
+                divide_and_store(step - 3)

@@ -34,13 +34,10 @@ def tile_selfattentionlayer_pa_kernel(tc, q, k, x, Wv, bv, out):
         inputs = ctx.enter_context(tc.tile_pool(name="inputs", bufs=1))
         operands = ctx.enter_context(tc.tile_pool(name="operands", bufs=1))
         grouped_pool = ctx.enter_context(tc.tile_pool(name="grouped", bufs=4))
-        angle_pool = ctx.enter_context(tc.tile_pool(name="angle", bufs=3))
         small = ctx.enter_context(tc.tile_pool(name="small", bufs=8))
-        e_pool = ctx.enter_context(tc.tile_pool(name="e", bufs=3))
         out_pool = ctx.enter_context(tc.tile_pool(name="out", bufs=3))
         tr_banks = ctx.enter_context(tc.psum_pool(name="tr_banks", bufs=2))
         acc_banks = ctx.enter_context(tc.psum_pool(name="acc_banks", bufs=6))
-        ctx.enter_context(tc.manual_schedule())
 
         ident = const.tile([P, P], F32, name="ident")
         make_identity(nc, ident[:])
@@ -53,22 +50,22 @@ def tile_selfattentionlayer_pa_kernel(tc, q, k, x, Wv, bv, out):
         warm = const.tile([P, 1], F32, name="warm")
         nc.scalar.activation(out=warm[:], in_=neg_half[:], func=ACT.Sin)
 
-        nc.sync.dma_start(out=bias_row[0:1, :], in_=bv.rearrange("(o d) -> o d", o=1))
-        wv_sb = inputs.tile([P, 4, FEATURES], BF16, name="wv_sb")
-        nc.sync.dma_start(out=wv_sb[:], in_=Wv.rearrange("(t p) d -> p t d", p=P))
-        x_sb = inputs.tile([P, 4, 2, FEATURES], BF16, name="x_sb")
         k_sb = inputs.tile([P, ROW_TILES, FEATURES], BF16, name="k_sb")
         q_sb = inputs.tile([P, ROW_TILES, FEATURES], BF16, name="q_sb")
-        for c in range(4):
-            nc.sync.dma_start(
-                out=x_sb[:, c, :, :], in_=x[c * 256 : (c + 1) * 256, :].rearrange("(p e) d -> p e d", e=2)
-            )
         for src, dst in ((k, k_sb), (q, q_sb)):
             for c in range(4):
                 nc.sync.dma_start(
                     out=dst[:, 2 * c : 2 * c + 2, :],
                     in_=src[c * 256 : (c + 1) * 256, :].rearrange("(t p) d -> p t d", p=P),
                 )
+        wv_sb = inputs.tile([P, 4, FEATURES], BF16, name="wv_sb")
+        nc.sync.dma_start(out=wv_sb[:], in_=Wv.rearrange("(t p) d -> p t d", p=P))
+        x_sb = inputs.tile([P, 4, 2, FEATURES], BF16, name="x_sb")
+        for c in range(4):
+            nc.sync.dma_start(
+                out=x_sb[:, c, :, :], in_=x[c * 256 : (c + 1) * 256, :].rearrange("(p e) d -> p e d", e=2)
+            )
+        nc.sync.dma_start(out=bias_row[0:1, :], in_=bv.rearrange("(o d) -> o d", o=1))
 
         def last_axis_to_partitions(block_a, block_b, grouped):
             bank = tr_banks.tile([P, 2, 2, P], F32, tag="tr", name="tr_bank")
@@ -100,6 +97,76 @@ def tile_selfattentionlayer_pa_kernel(tc, q, k, x, Wv, bv, out):
                     out=codes[:, cols].bitcast(FP8X4), scales=scales[:, cols], in_=grouped[:]
                 )
 
+        k_codes, k_scales = new_operand(ROWS, "k")
+        q_codes, q_scales = new_operand(ROWS, "q")
+        quantise_rows([k_sb[:, t, :] for t in range(ROW_TILES)], k_codes, k_scales)
+        quantise_rows([q_sb[:, t, :] for t in range(ROW_TILES)], q_codes, q_scales)
+        sines = operands.tile([P, ROW_TILES, ROWS], F32, name="sines")
+
+        def sine_of_standardised_scores(i, angle_pool):
+            queries = slice(i * P, (i + 1) * P)
+            s_banks = [acc_banks.tile([P, FEATURES], F32, tag="acc", name="s_bank%d" % h) for h in range(2)]
+            stats = small.tile([P, 2, 6], F32, name="stats")
+            for h in range(2):
+                keys = slice(h * 512, (h + 1) * 512)
+                nc.tensor.matmul_mx(
+                    out=s_banks[h][:],
+                    lhsT=q_codes[:, queries].bitcast(FP8X4),
+                    lhsT_scale=q_scales[:, queries],
+                    rhs=k_codes[:, keys].bitcast(FP8X4),
+                    rhs_scale=k_scales[:, keys],
+                    start=True,
+                    stop=True,
+                )
+                nc.vector.bn_stats(out=stats[:, h, :], in_=s_banks[h][:])
+            mean_var = small.tile([P, 2], F32, name="mean_var")
+            nc.vector.bn_aggr(out=mean_var[:], in_=stats[:].rearrange("p h s -> p (h s)"))
+            scaled_var = small.tile([P, 1], F32, name="scaled_var")
+            nc.vector.tensor_scalar(
+                out=scaled_var[:],
+                in0=mean_var[:, 1:2],
+                scalar1=TWO_PI * TWO_PI * ROWS / (ROWS - 1),
+                scalar2=TWO_PI * TWO_PI * EPS,
+                op0=ALU.mult,
+                op1=ALU.add,
+            )
+            turn_scale = small.tile([P, 1], F32, name="turn_scale")
+            nc.gpsimd.tensor_tensor(out=turn_scale[:], in0=scaled_var[:], in1=neg_half[:], op=ALU.pow)
+            turn_bias = small.tile([P, 1], F32, name="turn_bias")
+            nc.vector.tensor_scalar(
+                out=turn_bias[:],
+                in0=mean_var[:, 0:1],
+                scalar1=turn_scale[:, 0:1],
+                scalar2=-1.0,
+                op0=ALU.mult,
+                op1=ALU.mult,
+            )
+            turns = angle_pool.tile([P, ROWS], F32, name="turns")
+            for h in range(2):
+                nc.scalar.activation(
+                    out=turns[:, h * 512 : (h + 1) * 512],
+                    in_=s_banks[h][:],
+                    func=ACT.Identity,
+                    bias=turn_bias[:, 0:1],
+                    scale=turn_scale[:, 0:1],
+                )
+            shifted = angle_pool.tile([P, ROWS], F32, name="shifted")
+            nc.vector.tensor_scalar(out=shifted[:], in0=turns[:], scalar1=ROUND_MAGIC, scalar2=None, op0=ALU.add)
+            neg_frac = angle_pool.tile([P, ROWS], F32, name="neg_frac")
+            nc.vector.scalar_tensor_tensor(
+                out=neg_frac[:],
+                in0=shifted[:],
+                scalar=ROUND_MAGIC,
+                in1=turns[:],
+                op0=ALU.subtract,
+                op1=ALU.subtract,
+            )
+            nc.scalar.activation(out=sines[:, i, :], in_=neg_frac[:], func=ACT.Sin, scale=-TWO_PI)
+
+        with tc.tile_pool(name="angle", bufs=3) as angle_pool:
+            for i in range(ROW_TILES):
+                sine_of_standardised_scores(i, angle_pool)
+
         bias_bank = acc_banks.tile([P, FEATURES], F32, tag="acc", name="bias_bank")
         nc.tensor.matmul(out=bias_bank[:], lhsT=ones[:], rhs=bias_row[:], start=True, stop=True)
         bias_all = const.tile([P, FEATURES], F32, name="bias_all")
@@ -107,13 +174,12 @@ def tile_selfattentionlayer_pa_kernel(tc, q, k, x, Wv, bv, out):
 
         wv_codes, wv_scales = new_operand(FEATURES, "wv")
         x_codes, x_scales = new_operand(ROWS, "x")
-        k_codes, k_scales = new_operand(ROWS, "k")
-        q_codes, q_scales = new_operand(ROWS, "q")
+        quantise_rows([wv_sb[:, t, :] for t in range(4)], wv_codes, wv_scales)
+        quantise_rows([x_sb[:, c, e, :] for c in range(4) for e in range(2)], x_codes, x_scales)
         v_grouped = operands.tile([P, KEY_PASSES, FEATURES, PACK], BF16, align_bytes=64, name="v_grouped")
         v_codes = operands.tile([P, KEY_PASSES, FEATURES], U32, align_bytes=64, name="v_codes")
         v_scales = operands.tile([P, KEY_PASSES, FEATURES], U8, align_bytes=64, name="v_scales")
-
-        def value_pass(g):
+        for g in range(KEY_PASSES):
             for c in range(FEATURES // P):
                 feats = slice(c * P, (c + 1) * P)
                 v_bank = acc_banks.tile([P, PACK, P], F32, tag="acc", name="v_bank")
@@ -140,142 +206,35 @@ def tile_selfattentionlayer_pa_kernel(tc, q, k, x, Wv, bv, out):
                 in_=v_grouped[:, g, :, :].rearrange("p o j -> p (o j)"),
             )
 
-        quantise_rows([wv_sb[:, t, :] for t in range(4)], wv_codes, wv_scales)
-        quantise_rows([x_sb[:, c, e, :] for c in range(4) for e in range(2)], x_codes, x_scales)
-        value_pass(0)
-        quantise_rows([k_sb[:, t, :] for t in range(ROW_TILES)], k_codes, k_scales)
-        quantise_rows([q_sb[:, t, :] for t in range(ROW_TILES)], q_codes, q_scales)
-        value_pass(1)
-
-        sines = operands.tile([P, ROW_TILES, ROWS], F32, name="sines")
-        s_banks, turn_scale, turn_bias, mean_var, turns, neg_frac = {}, {}, {}, {}, {}, {}
-
-        def scores(i):
-            queries = slice(i * P, (i + 1) * P)
-            s_banks[i] = [
-                acc_banks.tile([P, FEATURES], F32, tag="acc", name="s_bank%d" % h) for h in range(2)
-            ]
-            for h in range(2):
-                keys = slice(h * 512, (h + 1) * 512)
-                nc.tensor.matmul_mx(
-                    out=s_banks[i][h][:],
-                    lhsT=q_codes[:, queries].bitcast(FP8X4),
-                    lhsT_scale=q_scales[:, queries],
-                    rhs=k_codes[:, keys].bitcast(FP8X4),
-                    rhs_scale=k_scales[:, keys],
-                    start=True,
-                    stop=True,
-                )
-
-        def row_statistics(i):
-            stats = small.tile([P, 2, 6], F32, name="stats")
-            for h in range(2):
-                nc.vector.bn_stats(out=stats[:, h, :], in_=s_banks[i][h][:])
-            mean_var[i] = small.tile([P, 2], F32, name="mean_var")
-            nc.vector.bn_aggr(out=mean_var[i][:], in_=stats[:].rearrange("p h s -> p (h s)"))
-            scaled_var = small.tile([P, 1], F32, name="scaled_var")
-            nc.vector.tensor_scalar(
-                out=scaled_var[:],
-                in0=mean_var[i][:, 1:2],
-                scalar1=TWO_PI * TWO_PI * ROWS / (ROWS - 1),
-                scalar2=TWO_PI * TWO_PI * EPS,
-                op0=ALU.mult,
-                op1=ALU.add,
-            )
-            turn_scale[i] = small.tile([P, 1], F32, name="turn_scale")
-            nc.gpsimd.tensor_tensor(out=turn_scale[i][:], in0=scaled_var[:], in1=neg_half[:], op=ALU.pow)
-
-        def angle_in_turns(i):
-            turn_bias[i] = small.tile([P, 1], F32, name="turn_bias")
-            nc.vector.tensor_scalar(
-                out=turn_bias[i][:],
-                in0=mean_var[i][:, 0:1],
-                scalar1=turn_scale[i][:, 0:1],
-                scalar2=-1.0,
-                op0=ALU.mult,
-                op1=ALU.mult,
-            )
-            turns[i] = angle_pool.tile([P, ROWS], F32, name="turns")
-            for h in range(2):
-                nc.scalar.activation(
-                    out=turns[i][:, h * 512 : (h + 1) * 512],
-                    in_=s_banks[i][h][:],
-                    func=ACT.Identity,
-                    bias=turn_bias[i][:, 0:1],
-                    scale=turn_scale[i][:, 0:1],
-                )
-
-        def drop_whole_turns(i):
-            shifted = angle_pool.tile([P, ROWS], F32, name="shifted")
-            nc.vector.tensor_scalar(
-                out=shifted[:], in0=turns[i][:], scalar1=ROUND_MAGIC, scalar2=None, op0=ALU.add
-            )
-            neg_frac[i] = angle_pool.tile([P, ROWS], F32, name="neg_frac")
-            nc.vector.scalar_tensor_tensor(
-                out=neg_frac[i][:],
-                in0=shifted[:],
-                scalar=ROUND_MAGIC,
-                in1=turns[i][:],
-                op0=ALU.subtract,
-                op1=ALU.subtract,
-            )
-
-        def sine(i):
-            nc.scalar.activation(out=sines[:, i, :], in_=neg_frac[i][:], func=ACT.Sin, scale=-TWO_PI)
-
-        scores(0)
-        scores(1)
-        scores(2)
-        row_statistics(0)
-        for i in range(ROW_TILES):
-            if i + 1 < ROW_TILES:
-                row_statistics(i + 1)
-            angle_in_turns(i)
-            if i + 3 < ROW_TILES:
-                scores(i + 3)
-            if i >= 1:
-                drop_whole_turns(i - 1)
-                sine(i - 1)
-        drop_whole_turns(ROW_TILES - 1)
-        sine(ROW_TILES - 1)
-
-        exp_bias, row_sum, e_rows, e_grouped, out_banks, inv_sum = {}, {}, {}, {}, {}, {}
-
-        def row_maximum(i):
+        def attend(i, e_pool):
             top = small.tile([P, 1], F32, name="top")
             nc.vector.tensor_reduce(out=top[:], in_=sines[:, i, :], axis=AXIS.X, op=ALU.max)
-            exp_bias[i] = small.tile([P, 1], F32, name="exp_bias")
+            exp_bias = small.tile([P, 1], F32, name="exp_bias")
             nc.vector.tensor_scalar(
-                out=exp_bias[i][:], in0=top[:], scalar1=-INV_SQRT_FEATURES, scalar2=None, op0=ALU.mult
+                out=exp_bias[:], in0=top[:], scalar1=-INV_SQRT_FEATURES, scalar2=None, op0=ALU.mult
             )
-
-        def exponential(i):
-            e_rows[i] = e_pool.tile([P, ROWS], BF16, name="e_rows")
-            row_sum[i] = small.tile([P, 1], F32, name="row_sum")
+            e_rows = e_pool.tile([P, ROWS], BF16, name="e_rows")
+            row_sum = small.tile([P, 1], F32, name="row_sum")
             nc.scalar.activation(
-                out=e_rows[i][:],
+                out=e_rows[:],
                 in_=sines[:, i, :],
                 func=ACT.Exp,
-                bias=exp_bias[i][:, 0:1],
+                bias=exp_bias[:, 0:1],
                 scale=INV_SQRT_FEATURES,
-                accum_out=row_sum[i][:, 0:1],
+                accum_out=row_sum[:, 0:1],
             )
-
-        def keys_to_partitions(i):
-            e_grouped[i] = new_grouped()
-            last_axis_to_partitions(e_rows[i][:, 0:512], e_rows[i][:, 512:1024], e_grouped[i][:])
-
-        def weighted_sum(i):
-            inv_sum[i] = small.tile([P, 1], F32, name="inv_sum")
-            nc.vector.reciprocal(out=inv_sum[i][:], in_=row_sum[i][:])
+            inv_sum = small.tile([P, 1], F32, name="inv_sum")
+            nc.vector.reciprocal(out=inv_sum[:], in_=row_sum[:])
+            e_grouped = new_grouped()
+            last_axis_to_partitions(e_rows[:, 0:512], e_rows[:, 512:1024], e_grouped[:])
             e_codes = e_pool.tile([P, KEY_PASSES * P], U32, align_bytes=64, name="e_codes")
             e_scales = e_pool.tile([P, KEY_PASSES * P], U8, align_bytes=64, name="e_scales")
-            nc.vector.quantize_mx(out=e_codes[:].bitcast(FP8X4), scales=e_scales[:], in_=e_grouped[i][:])
-            out_banks[i] = acc_banks.tile([P, FEATURES], F32, tag="acc", name="out_bank")
+            nc.vector.quantize_mx(out=e_codes[:].bitcast(FP8X4), scales=e_scales[:], in_=e_grouped[:])
+            out_bank = acc_banks.tile([P, FEATURES], F32, tag="acc", name="out_bank")
             for g in range(KEY_PASSES):
                 queries = slice(g * P, (g + 1) * P)
                 nc.tensor.matmul_mx(
-                    out=out_banks[i][:],
+                    out=out_bank[:],
                     lhsT=e_codes[:, queries].bitcast(FP8X4),
                     lhsT_scale=e_scales[:, queries],
                     rhs=v_codes[:, g, :].bitcast(FP8X4),
@@ -283,24 +242,12 @@ def tile_selfattentionlayer_pa_kernel(tc, q, k, x, Wv, bv, out):
                     start=(g == 0),
                     stop=(g == KEY_PASSES - 1),
                 )
-
-        def divide_and_store(i):
             result = out_pool.tile([P, FEATURES], F32, name="result")
             nc.vector.tensor_scalar(
-                out=result[:], in0=out_banks[i][:], scalar1=inv_sum[i][:, 0:1], scalar2=None, op0=ALU.mult
+                out=result[:], in0=out_bank[:], scalar1=inv_sum[:, 0:1], scalar2=None, op0=ALU.mult
             )
             nc.sync.dma_start(out=out[i * P : (i + 1) * P, :], in_=result[:])
 
-        row_maximum(0)
-        row_maximum(1)
-        for step in range(ROW_TILES + 3):
-            if step < ROW_TILES:
-                exponential(step)
-            if step + 2 < ROW_TILES:
-                row_maximum(step + 2)
-            if 0 <= step - 1 < ROW_TILES:
-                keys_to_partitions(step - 1)
-            if 0 <= step - 2 < ROW_TILES:
-                weighted_sum(step - 2)
-            if 0 <= step - 3 < ROW_TILES:
-                divide_and_store(step - 3)
+        with tc.tile_pool(name="e", bufs=3) as e_pool:
+            for i in range(ROW_TILES):
+                attend(i, e_pool)

@@ -151,7 +151,9 @@ def tile_selfattentionlayer_pa_kernel(tc, q, k, x, Wv, bv, out):
                     scale=turn_scale[:, 0:1],
                 )
             shifted = angle_pool.tile([P, ROWS], F32, name="shifted")
-            nc.vector.tensor_scalar(out=shifted[:], in0=turns[:], scalar1=ROUND_MAGIC, scalar2=None, op0=ALU.add)
+            nc.gpsimd.tensor_scalar(
+                out=shifted[:], in0=turns[:], scalar1=1.0, scalar2=ROUND_MAGIC, op0=ALU.mult, op1=ALU.add
+            )
             neg_frac = angle_pool.tile([P, ROWS], F32, name="neg_frac")
             nc.vector.scalar_tensor_tensor(
                 out=neg_frac[:],

@@ -47,6 +47,8 @@ def tile_selfattentionlayer_pa_kernel(tc, q, k, x, Wv, bv, out):
         nc.vector.memset(bias_row[:], 0.0)
         neg_half = const.tile([P, 1], F32, name="neg_half")
         nc.vector.memset(neg_half[:], -0.5)
+        magic = const.tile([P, 1], F32, name="magic")
+        nc.vector.memset(magic[:], ROUND_MAGIC)
         warm = const.tile([P, 1], F32, name="warm")
         nc.scalar.activation(out=warm[:], in_=neg_half[:], func=ACT.Sin)
 
@@ -67,7 +69,7 @@ def tile_selfattentionlayer_pa_kernel(tc, q, k, x, Wv, bv, out):
             )
         nc.sync.dma_start(out=bias_row[0:1, :], in_=bv.rearrange("(o d) -> o d", o=1))
 
-        def last_axis_to_partitions(block_a, block_b, grouped):
+        def last_axis_to_partitions(block_a, block_b, grouped, on_vector=False):
             bank = tr_banks.tile([P, 2, 2, P], F32, tag="tr", name="tr_bank")
             for b, block in enumerate((block_a, block_b)):
                 words = block.bitcast(F32)
@@ -75,7 +77,8 @@ def tile_selfattentionlayer_pa_kernel(tc, q, k, x, Wv, bv, out):
                     nc.tensor.transpose(
                         out=bank[:, b, u, :], in_=words[:, u * P : (u + 1) * P], identity=ident[:]
                     )
-            nc.scalar.copy(
+            copy = nc.vector.tensor_copy if on_vector else nc.scalar.copy
+            copy(
                 out=grouped.bitcast(F32).rearrange("p (b r u) -> p b r u", b=2, u=2),
                 in_=bank[:].rearrange("p b u r -> p b r u"),
             )
@@ -151,9 +154,12 @@ def tile_selfattentionlayer_pa_kernel(tc, q, k, x, Wv, bv, out):
                     scale=turn_scale[:, 0:1],
                 )
             shifted = angle_pool.tile([P, ROWS], F32, name="shifted")
-            nc.gpsimd.tensor_scalar(
-                out=shifted[:], in0=turns[:], scalar1=1.0, scalar2=ROUND_MAGIC, op0=ALU.mult, op1=ALU.add
-            )
+            if i % 2 == 0:
+                nc.vector.tensor_scalar(
+                    out=shifted[:], in0=turns[:], scalar1=ROUND_MAGIC, scalar2=None, op0=ALU.add
+                )
+            else:
+                nc.scalar.activation(out=shifted[:], in_=turns[:], func=ACT.Identity, bias=magic[:, 0:1])
             neg_frac = angle_pool.tile([P, ROWS], F32, name="neg_frac")
             nc.vector.scalar_tensor_tensor(
                 out=neg_frac[:],
@@ -228,7 +234,7 @@ def tile_selfattentionlayer_pa_kernel(tc, q, k, x, Wv, bv, out):
             inv_sum = small.tile([P, 1], F32, name="inv_sum")
             nc.vector.reciprocal(out=inv_sum[:], in_=row_sum[:])
             e_grouped = new_grouped()
-            last_axis_to_partitions(e_rows[:, 0:512], e_rows[:, 512:1024], e_grouped[:])
+            last_axis_to_partitions(e_rows[:, 0:512], e_rows[:, 512:1024], e_grouped[:], on_vector=(i % 2 == 1))
             e_codes = e_pool.tile([P, KEY_PASSES * P], U32, align_bytes=64, name="e_codes")
             e_scales = e_pool.tile([P, KEY_PASSES * P], U8, align_bytes=64, name="e_scales")
             nc.vector.quantize_mx(out=e_codes[:].bitcast(FP8X4), scales=e_scales[:], in_=e_grouped[:])
@@ -245,9 +251,12 @@ def tile_selfattentionlayer_pa_kernel(tc, q, k, x, Wv, bv, out):
                     stop=(g == KEY_PASSES - 1),
                 )
             result = out_pool.tile([P, FEATURES], F32, name="result")
-            nc.vector.tensor_scalar(
-                out=result[:], in0=out_bank[:], scalar1=inv_sum[:, 0:1], scalar2=None, op0=ALU.mult
-            )
+            if i % 2 == 1:
+                nc.vector.tensor_scalar(
+                    out=result[:], in0=out_bank[:], scalar1=inv_sum[:, 0:1], scalar2=None, op0=ALU.mult
+                )
+            else:
+                nc.scalar.activation(out=result[:], in_=out_bank[:], func=ACT.Copy, scale=inv_sum[:, 0:1])
             nc.sync.dma_start(out=out[i * P : (i + 1) * P, :], in_=result[:])
 
         with tc.tile_pool(name="e", bufs=3) as e_pool:

@@ -33,11 +33,14 @@ def tile_selfattentionlayer_pa_kernel(tc, q, k, x, Wv, bv, out):
         const = ctx.enter_context(tc.tile_pool(name="const", bufs=1))
         inputs = ctx.enter_context(tc.tile_pool(name="inputs", bufs=1))
         operands = ctx.enter_context(tc.tile_pool(name="operands", bufs=1))
-        grouped_pool = ctx.enter_context(tc.tile_pool(name="grouped", bufs=4))
+        grouped_pool = ctx.enter_context(tc.tile_pool(name="grouped", bufs=6))
+        angles = ctx.enter_context(tc.tile_pool(name="angles", bufs=4))
+        e_pool = ctx.enter_context(tc.tile_pool(name="e", bufs=4))
         small = ctx.enter_context(tc.tile_pool(name="small", bufs=8))
         out_pool = ctx.enter_context(tc.tile_pool(name="out", bufs=3))
         tr_banks = ctx.enter_context(tc.psum_pool(name="tr_banks", bufs=2))
         acc_banks = ctx.enter_context(tc.psum_pool(name="acc_banks", bufs=6))
+        ctx.enter_context(tc.manual_schedule())
 
         ident = const.tile([P, P], F32, name="ident")
         make_identity(nc, ident[:])
@@ -47,19 +50,16 @@ def tile_selfattentionlayer_pa_kernel(tc, q, k, x, Wv, bv, out):
         nc.vector.memset(bias_row[:], 0.0)
         neg_half = const.tile([P, 1], F32, name="neg_half")
         nc.vector.memset(neg_half[:], -0.5)
-        magic = const.tile([P, 1], F32, name="magic")
-        nc.vector.memset(magic[:], ROUND_MAGIC)
         warm = const.tile([P, 1], F32, name="warm")
         nc.scalar.activation(out=warm[:], in_=neg_half[:], func=ACT.Sin)
 
         k_sb = inputs.tile([P, ROW_TILES, FEATURES], BF16, name="k_sb")
         q_sb = inputs.tile([P, ROW_TILES, FEATURES], BF16, name="q_sb")
-        for src, dst in ((k, k_sb), (q, q_sb)):
-            for c in range(4):
-                nc.sync.dma_start(
-                    out=dst[:, 2 * c : 2 * c + 2, :],
-                    in_=src[c * 256 : (c + 1) * 256, :].rearrange("(t p) d -> p t d", p=P),
-                )
+        for src, dst, c in [(q, q_sb, 0)] + [(k, k_sb, c) for c in range(4)] + [(q, q_sb, c) for c in range(1, 4)]:
+            nc.sync.dma_start(
+                out=dst[:, 2 * c : 2 * c + 2, :],
+                in_=src[c * 256 : (c + 1) * 256, :].rearrange("(t p) d -> p t d", p=P),
+            )
         wv_sb = inputs.tile([P, 4, FEATURES], BF16, name="wv_sb")
         nc.sync.dma_start(out=wv_sb[:], in_=Wv.rearrange("(t p) d -> p t d", p=P))
         x_sb = inputs.tile([P, 4, 2, FEATURES], BF16, name="x_sb")
@@ -69,7 +69,7 @@ def tile_selfattentionlayer_pa_kernel(tc, q, k, x, Wv, bv, out):
             )
         nc.sync.dma_start(out=bias_row[0:1, :], in_=bv.rearrange("(o d) -> o d", o=1))
 
-        def last_axis_to_partitions(block_a, block_b, grouped, on_vector=False):
+        def transpose_pair(block_a, block_b):
             bank = tr_banks.tile([P, 2, 2, P], F32, tag="tr", name="tr_bank")
             for b, block in enumerate((block_a, block_b)):
                 words = block.bitcast(F32)
@@ -77,43 +77,55 @@ def tile_selfattentionlayer_pa_kernel(tc, q, k, x, Wv, bv, out):
                     nc.tensor.transpose(
                         out=bank[:, b, u, :], in_=words[:, u * P : (u + 1) * P], identity=ident[:]
                     )
-            copy = nc.vector.tensor_copy if on_vector else nc.scalar.copy
+            return bank
+
+        def group_words(copy, bank):
+            grouped = grouped_pool.tile([P, 2 * P * PACK], BF16, align_bytes=64, tag="grouped", name="grouped")
             copy(
-                out=grouped.bitcast(F32).rearrange("p (b r u) -> p b r u", b=2, u=2),
+                out=grouped[:].bitcast(F32).rearrange("p (b r u) -> p b r u", b=2, u=2),
                 in_=bank[:].rearrange("p b u r -> p b r u"),
             )
-
-        def new_grouped():
-            return grouped_pool.tile([P, 2 * P * PACK], BF16, align_bytes=64, tag="grouped", name="grouped")
+            return grouped
 
         def new_operand(columns, name):
             codes = operands.tile([P, columns], U32, align_bytes=64, name=name + "_codes")
             scales = operands.tile([P, columns], U8, align_bytes=64, name=name + "_scales")
             return codes, scales
 
-        def quantise_rows(blocks, codes, scales):
-            for c in range(len(blocks) // 2):
-                grouped = new_grouped()
-                last_axis_to_partitions(blocks[2 * c], blocks[2 * c + 1], grouped[:])
-                cols = slice(c * 2 * P, (c + 1) * 2 * P)
-                nc.vector.quantize_mx(
-                    out=codes[:, cols].bitcast(FP8X4), scales=scales[:, cols], in_=grouped[:]
-                )
+        def quantise(grouped, codes, scales, c):
+            cols = slice(c * 2 * P, (c + 1) * 2 * P)
+            nc.vector.quantize_mx(out=codes[:, cols].bitcast(FP8X4), scales=scales[:, cols], in_=grouped[:])
 
         k_codes, k_scales = new_operand(ROWS, "k")
         q_codes, q_scales = new_operand(ROWS, "q")
-        quantise_rows([k_sb[:, t, :] for t in range(ROW_TILES)], k_codes, k_scales)
-        quantise_rows([q_sb[:, t, :] for t in range(ROW_TILES)], q_codes, q_scales)
+        wv_codes, wv_scales = new_operand(FEATURES, "wv")
+        x_codes, x_scales = new_operand(ROWS, "x")
         sines = operands.tile([P, ROW_TILES, ROWS], F32, name="sines")
+        v_grouped = operands.tile([P, KEY_PASSES, FEATURES, PACK], BF16, align_bytes=64, name="v_grouped")
+        v_codes = operands.tile([P, KEY_PASSES, FEATURES], U32, align_bytes=64, name="v_codes")
+        v_scales = operands.tile([P, KEY_PASSES, FEATURES], U8, align_bytes=64, name="v_scales")
 
-        def sine_of_standardised_scores(i, angle_pool):
+        def blocks_of(name, c):
+            if name == "k":
+                return k_sb[:, 2 * c, :], k_sb[:, 2 * c + 1, :], k_codes, k_scales
+            if name == "q":
+                return q_sb[:, 2 * c, :], q_sb[:, 2 * c + 1, :], q_codes, q_scales
+            if name == "w":
+                return wv_sb[:, 2 * c, :], wv_sb[:, 2 * c + 1, :], wv_codes, wv_scales
+            return x_sb[:, c, 0, :], x_sb[:, c, 1, :], x_codes, x_scales
+
+        on_scalar, on_vector = nc.scalar.copy, nc.vector.tensor_copy
+
+        s_banks, turn_scale, turn_bias, mean_var, halves, turns, shifted, neg_frac = {}, {}, {}, {}, {}, {}, {}, {}
+
+        def scores(i):
             queries = slice(i * P, (i + 1) * P)
-            s_banks = [acc_banks.tile([P, FEATURES], F32, tag="acc", name="s_bank%d" % h) for h in range(2)]
-            stats = small.tile([P, 2, 6], F32, name="stats")
+            s_banks[i] = []
             for h in range(2):
                 keys = slice(h * 512, (h + 1) * 512)
+                bank = acc_banks.tile([P, FEATURES], F32, tag="acc", name="s_bank")
                 nc.tensor.matmul_mx(
-                    out=s_banks[h][:],
+                    out=bank[:],
                     lhsT=q_codes[:, queries].bitcast(FP8X4),
                     lhsT_scale=q_scales[:, queries],
                     rhs=k_codes[:, keys].bitcast(FP8X4),
@@ -121,144 +133,262 @@ def tile_selfattentionlayer_pa_kernel(tc, q, k, x, Wv, bv, out):
                     start=True,
                     stop=True,
                 )
-                nc.vector.bn_stats(out=stats[:, h, :], in_=s_banks[h][:])
-            mean_var = small.tile([P, 2], F32, name="mean_var")
-            nc.vector.bn_aggr(out=mean_var[:], in_=stats[:].rearrange("p h s -> p (h s)"))
+                s_banks[i].append(bank)
+
+        def statistics(i):
+            stats = small.tile([P, 2, 6], F32, name="stats")
+            for h in range(2):
+                nc.vector.bn_stats(out=stats[:, h, :], in_=s_banks[i][h][:])
+            halves[i] = stats
+
+        def mean_and_variance(i):
+            mean_var[i] = small.tile([P, 2], F32, name="mean_var")
+            nc.vector.bn_aggr(out=mean_var[i][:], in_=halves[i][:].rearrange("p h s -> p (h s)"))
+
+        def turn_factors(i):
             scaled_var = small.tile([P, 1], F32, name="scaled_var")
-            nc.vector.tensor_scalar(
+            nc.gpsimd.tensor_scalar(
                 out=scaled_var[:],
-                in0=mean_var[:, 1:2],
+                in0=mean_var[i][:, 1:2],
                 scalar1=TWO_PI * TWO_PI * ROWS / (ROWS - 1),
                 scalar2=TWO_PI * TWO_PI * EPS,
                 op0=ALU.mult,
                 op1=ALU.add,
             )
-            turn_scale = small.tile([P, 1], F32, name="turn_scale")
-            nc.gpsimd.tensor_tensor(out=turn_scale[:], in0=scaled_var[:], in1=neg_half[:], op=ALU.pow)
-            turn_bias = small.tile([P, 1], F32, name="turn_bias")
-            nc.vector.tensor_scalar(
-                out=turn_bias[:],
-                in0=mean_var[:, 0:1],
-                scalar1=turn_scale[:, 0:1],
+            turn_scale[i] = small.tile([P, 1], F32, name="turn_scale")
+            nc.gpsimd.tensor_tensor(out=turn_scale[i][:], in0=scaled_var[:], in1=neg_half[:], op=ALU.pow)
+            turn_bias[i] = small.tile([P, 1], F32, name="turn_bias")
+            nc.gpsimd.tensor_scalar(
+                out=turn_bias[i][:],
+                in0=mean_var[i][:, 0:1],
+                scalar1=turn_scale[i][:, 0:1],
                 scalar2=-1.0,
                 op0=ALU.mult,
                 op1=ALU.mult,
             )
-            turns = angle_pool.tile([P, ROWS], F32, name="turns")
+
+        def to_turns(i):
+            turns[i] = angles.tile([P, ROWS], F32, name="turns")
             for h in range(2):
                 nc.scalar.activation(
-                    out=turns[:, h * 512 : (h + 1) * 512],
-                    in_=s_banks[h][:],
+                    out=turns[i][:, h * 512 : (h + 1) * 512],
+                    in_=s_banks[i][h][:],
                     func=ACT.Identity,
-                    bias=turn_bias[:, 0:1],
-                    scale=turn_scale[:, 0:1],
+                    bias=turn_bias[i][:, 0:1],
+                    scale=turn_scale[i][:, 0:1],
                 )
-            shifted = angle_pool.tile([P, ROWS], F32, name="shifted")
-            if i % 2 == 0:
-                nc.vector.tensor_scalar(
-                    out=shifted[:], in0=turns[:], scalar1=ROUND_MAGIC, scalar2=None, op0=ALU.add
-                )
-            else:
-                nc.scalar.activation(out=shifted[:], in_=turns[:], func=ACT.Identity, bias=magic[:, 0:1])
-            neg_frac = angle_pool.tile([P, ROWS], F32, name="neg_frac")
+
+        def shift(i):
+            shifted[i] = angles.tile([P, ROWS], F32, name="shifted")
+            nc.gpsimd.tensor_scalar(
+                out=shifted[i][:], in0=turns[i][:], scalar1=1.0, scalar2=ROUND_MAGIC, op0=ALU.mult, op1=ALU.add
+            )
+
+        def fraction(i):
+            neg_frac[i] = angles.tile([P, ROWS], F32, name="neg_frac")
             nc.vector.scalar_tensor_tensor(
-                out=neg_frac[:],
-                in0=shifted[:],
+                out=neg_frac[i][:],
+                in0=shifted[i][:],
                 scalar=ROUND_MAGIC,
-                in1=turns[:],
+                in1=turns[i][:],
                 op0=ALU.subtract,
                 op1=ALU.subtract,
             )
-            nc.scalar.activation(out=sines[:, i, :], in_=neg_frac[:], func=ACT.Sin, scale=-TWO_PI)
 
-        with tc.tile_pool(name="angle", bufs=3) as angle_pool:
-            for i in range(ROW_TILES):
-                sine_of_standardised_scores(i, angle_pool)
+        def sine(i):
+            nc.scalar.activation(out=sines[:, i, :], in_=neg_frac[i][:], func=ACT.Sin, scale=-TWO_PI)
 
-        bias_bank = acc_banks.tile([P, FEATURES], F32, tag="acc", name="bias_bank")
-        nc.tensor.matmul(out=bias_bank[:], lhsT=ones[:], rhs=bias_row[:], start=True, stop=True)
-        bias_all = const.tile([P, FEATURES], F32, name="bias_all")
-        nc.scalar.copy(out=bias_all[:], in_=bias_bank[:])
+        v_banks = {}
 
-        wv_codes, wv_scales = new_operand(FEATURES, "wv")
-        x_codes, x_scales = new_operand(ROWS, "x")
-        quantise_rows([wv_sb[:, t, :] for t in range(4)], wv_codes, wv_scales)
-        quantise_rows([x_sb[:, c, e, :] for c in range(4) for e in range(2)], x_codes, x_scales)
-        v_grouped = operands.tile([P, KEY_PASSES, FEATURES, PACK], BF16, align_bytes=64, name="v_grouped")
-        v_codes = operands.tile([P, KEY_PASSES, FEATURES], U32, align_bytes=64, name="v_codes")
-        v_scales = operands.tile([P, KEY_PASSES, FEATURES], U8, align_bytes=64, name="v_scales")
-        for g in range(KEY_PASSES):
-            for c in range(FEATURES // P):
-                feats = slice(c * P, (c + 1) * P)
-                v_bank = acc_banks.tile([P, PACK, P], F32, tag="acc", name="v_bank")
-                for j in range(PACK):
-                    rows = slice((PACK * g + j) * P, (PACK * g + j + 1) * P)
-                    nc.tensor.matmul_mx(
-                        out=v_bank[:, j, :],
-                        lhsT=x_codes[:, rows].bitcast(FP8X4),
-                        lhsT_scale=x_scales[:, rows],
-                        rhs=wv_codes[:, feats].bitcast(FP8X4),
-                        rhs_scale=wv_scales[:, feats],
-                        start=True,
-                        stop=True,
-                    )
-                nc.vector.tensor_tensor(
-                    out=v_grouped[:, g, feats, :],
-                    in0=v_bank[:].rearrange("p j o -> p o j"),
-                    in1=bias_all[:, feats].unsqueeze(2).to_broadcast([P, P, PACK]),
-                    op=ALU.add,
+        def v_products(b):
+            g, c = divmod(b, FEATURES // P)
+            feats = slice(c * P, (c + 1) * P)
+            v_banks[b] = acc_banks.tile([P, PACK, P], F32, tag="acc", name="v_bank")
+            for j in range(PACK):
+                rows = slice((PACK * g + j) * P, (PACK * g + j + 1) * P)
+                nc.tensor.matmul_mx(
+                    out=v_banks[b][:, j, :],
+                    lhsT=x_codes[:, rows].bitcast(FP8X4),
+                    lhsT_scale=x_scales[:, rows],
+                    rhs=wv_codes[:, feats].bitcast(FP8X4),
+                    rhs_scale=wv_scales[:, feats],
+                    start=True,
+                    stop=True,
                 )
+
+        def v_add(b):
+            g, c = divmod(b, FEATURES // P)
+            feats = slice(c * P, (c + 1) * P)
+            nc.vector.tensor_tensor(
+                out=v_grouped[:, g, feats, :],
+                in0=v_banks[b][:].rearrange("p j o -> p o j"),
+                in1=bias_all[:, feats].unsqueeze(2).to_broadcast([P, P, PACK]),
+                op=ALU.add,
+            )
+
+        def v_quantise(g):
             nc.vector.quantize_mx(
                 out=v_codes[:, g, :].bitcast(FP8X4),
                 scales=v_scales[:, g, :],
                 in_=v_grouped[:, g, :, :].rearrange("p o j -> p (o j)"),
             )
 
-        def attend(i, e_pool):
+        exp_bias, e_rows, row_sum, inv_sum, e_banks, e_grouped, e_ops, out_banks = {}, {}, {}, {}, {}, {}, {}, {}
+
+        def row_max(i):
             top = small.tile([P, 1], F32, name="top")
             nc.vector.tensor_reduce(out=top[:], in_=sines[:, i, :], axis=AXIS.X, op=ALU.max)
-            exp_bias = small.tile([P, 1], F32, name="exp_bias")
-            nc.vector.tensor_scalar(
-                out=exp_bias[:], in0=top[:], scalar1=-INV_SQRT_FEATURES, scalar2=None, op0=ALU.mult
+            exp_bias[i] = small.tile([P, 1], F32, name="exp_bias")
+            nc.gpsimd.tensor_scalar(
+                out=exp_bias[i][:], in0=top[:], scalar1=-INV_SQRT_FEATURES, scalar2=0.0, op0=ALU.mult, op1=ALU.add
             )
-            e_rows = e_pool.tile([P, ROWS], BF16, name="e_rows")
-            row_sum = small.tile([P, 1], F32, name="row_sum")
+
+        def exponential(i):
+            e_rows[i] = e_pool.tile([P, ROWS], BF16, name="e_rows")
+            row_sum[i] = small.tile([P, 1], F32, name="row_sum")
             nc.scalar.activation(
-                out=e_rows[:],
+                out=e_rows[i][:],
                 in_=sines[:, i, :],
                 func=ACT.Exp,
-                bias=exp_bias[:, 0:1],
+                bias=exp_bias[i][:, 0:1],
                 scale=INV_SQRT_FEATURES,
-                accum_out=row_sum[:, 0:1],
+                accum_out=row_sum[i][:, 0:1],
             )
-            inv_sum = small.tile([P, 1], F32, name="inv_sum")
-            nc.vector.reciprocal(out=inv_sum[:], in_=row_sum[:])
-            e_grouped = new_grouped()
-            last_axis_to_partitions(e_rows[:, 0:512], e_rows[:, 512:1024], e_grouped[:], on_vector=(i % 2 == 1))
-            e_codes = e_pool.tile([P, KEY_PASSES * P], U32, align_bytes=64, name="e_codes")
-            e_scales = e_pool.tile([P, KEY_PASSES * P], U8, align_bytes=64, name="e_scales")
-            nc.vector.quantize_mx(out=e_codes[:].bitcast(FP8X4), scales=e_scales[:], in_=e_grouped[:])
-            out_bank = acc_banks.tile([P, FEATURES], F32, tag="acc", name="out_bank")
+
+        def invert_sum(i):
+            inv_sum[i] = small.tile([P, 1], F32, name="inv_sum")
+            nc.vector.reciprocal(out=inv_sum[i][:], in_=row_sum[i][:])
+
+        def e_quantise(i):
+            codes = e_pool.tile([P, KEY_PASSES * P], U32, align_bytes=64, name="e_codes")
+            scales = e_pool.tile([P, KEY_PASSES * P], U8, align_bytes=64, name="e_scales")
+            nc.vector.quantize_mx(out=codes[:].bitcast(FP8X4), scales=scales[:], in_=e_grouped[i][:])
+            e_ops[i] = (codes, scales)
+
+        def e_times_v(i):
+            codes, scales = e_ops[i]
+            out_banks[i] = acc_banks.tile([P, FEATURES], F32, tag="acc", name="out_bank")
             for g in range(KEY_PASSES):
                 queries = slice(g * P, (g + 1) * P)
                 nc.tensor.matmul_mx(
-                    out=out_bank[:],
-                    lhsT=e_codes[:, queries].bitcast(FP8X4),
-                    lhsT_scale=e_scales[:, queries],
+                    out=out_banks[i][:],
+                    lhsT=codes[:, queries].bitcast(FP8X4),
+                    lhsT_scale=scales[:, queries],
                     rhs=v_codes[:, g, :].bitcast(FP8X4),
                     rhs_scale=v_scales[:, g, :],
                     start=(g == 0),
                     stop=(g == KEY_PASSES - 1),
                 )
+
+        def finish(i, on_vec):
             result = out_pool.tile([P, FEATURES], F32, name="result")
-            if i % 2 == 1:
+            if on_vec:
                 nc.vector.tensor_scalar(
-                    out=result[:], in0=out_bank[:], scalar1=inv_sum[:, 0:1], scalar2=None, op0=ALU.mult
+                    out=result[:], in0=out_banks[i][:], scalar1=inv_sum[i][:, 0:1], scalar2=None, op0=ALU.mult
                 )
             else:
-                nc.scalar.activation(out=result[:], in_=out_bank[:], func=ACT.Copy, scale=inv_sum[:, 0:1])
+                nc.scalar.activation(out=result[:], in_=out_banks[i][:], func=ACT.Copy, scale=inv_sum[i][:, 0:1])
             nc.sync.dma_start(out=out[i * P : (i + 1) * P, :], in_=result[:])
 
-        with tc.tile_pool(name="e", bufs=3) as e_pool:
-            for i in range(ROW_TILES):
-                attend(i, e_pool)
+        pending = []
+
+        def fetch(name, c, copy):
+            block_a, block_b, codes, scales = blocks_of(name, c)
+            pending.append((group_words(copy, transpose_pair(block_a, block_b)), codes, scales, c))
+
+        def settle():
+            quantise(*pending.pop(0))
+
+        fetch("q", 0, on_scalar)
+        fetch("k", 0, on_vector)
+        settle()
+        fetch("k", 1, on_scalar)
+        settle()
+        fetch("k", 2, on_vector)
+        settle()
+        fetch("k", 3, on_scalar)
+        settle()
+        settle()
+        fetch("q", 1, on_scalar)
+        scores(0)
+        fetch("q", 2, on_scalar)
+        statistics(0)
+        settle()
+        mean_and_variance(0)
+        turn_factors(0)
+        fetch("q", 3, on_scalar)
+        scores(1)
+        fetch("w", 0, on_scalar)
+        statistics(1)
+        settle()
+        mean_and_variance(1)
+        turn_factors(1)
+        scores(2)
+        fetch("w", 1, on_scalar)
+        to_turns(0)
+        shift(0)
+        statistics(2)
+        settle()
+        mean_and_variance(2)
+        turn_factors(2)
+        fetch("x", 0, on_scalar)
+        scores(3)
+        to_turns(1)
+        settle()
+
+        for i in range(ROW_TILES):
+            if i + 3 < ROW_TILES:
+                statistics(i + 3)
+            if i > 0:
+                sine(i - 1)
+            if i + 2 < ROW_TILES:
+                to_turns(i + 2)
+            if i + 1 < ROW_TILES:
+                shift(i + 1)
+            if i == ROW_TILES - 2:
+                row_max(0)
+            fraction(i)
+            if i + 3 < ROW_TILES:
+                mean_and_variance(i + 3)
+                turn_factors(i + 3)
+            if pending:
+                settle()
+            if i + 4 < ROW_TILES:
+                scores(i + 4)
+            if i < 3:
+                fetch("x", i + 1, on_scalar)
+            if i == 4:
+                bias_bank = acc_banks.tile([P, FEATURES], F32, tag="acc", name="bias_bank")
+                nc.tensor.matmul(out=bias_bank[:], lhsT=ones[:], rhs=bias_row[:], start=True, stop=True)
+                bias_all = const.tile([P, FEATURES], F32, name="bias_all")
+                nc.scalar.copy(out=bias_all[:], in_=bias_bank[:])
+        sine(ROW_TILES - 1)
+
+        row_max(1)
+        for b in range(4):
+            v_products(b)
+        for b in range(4):
+            v_add(b)
+            v_products(b + 4)
+        row_max(2)
+        v_quantise(0)
+
+        for j in range(ROW_TILES + 1 + 1):
+            if j < ROW_TILES:
+                exponential(j)
+                e_banks[j] = transpose_pair(e_rows[j][:, 0:512], e_rows[j][:, 512:1024])
+            if j in (0, 1):
+                v_add(2 * j + 4)
+                v_add(2 * j + 5)
+            if j + 3 < ROW_TILES:
+                row_max(j + 3)
+            if j == 1:
+                v_quantise(1)
+            if 1 <= j <= ROW_TILES:
+                e_grouped[j - 1] = group_words(on_vector if j - 1 in (4, 5, 6, 7) else on_scalar, e_banks[j - 1])
+                invert_sum(j - 1)
+            if 1 <= j < ROW_TILES + 1:
+                e_quantise(j - 1)
+                e_times_v(j - 1)
+            if j >= 1 + 1:
+                finish(j - 1 - 1, j - 1 - 1 in (0, 2, 4, 6))

@@ -38,9 +38,7 @@ def tile_selfattentionlayer_pa_kernel(tc, q, k, x, Wv, bv, out):
         e_pool = ctx.enter_context(tc.tile_pool(name="e", bufs=4))
         small = ctx.enter_context(tc.tile_pool(name="small", bufs=8))
         out_pool = ctx.enter_context(tc.tile_pool(name="out", bufs=3))
-        tr_banks = ctx.enter_context(tc.psum_pool(name="tr_banks", bufs=2))
-        acc_banks = ctx.enter_context(tc.psum_pool(name="acc_banks", bufs=6))
-        ctx.enter_context(tc.manual_schedule())
+        acc_banks = ctx.enter_context(tc.psum_pool(name="acc_banks", bufs=8))
 
         ident = const.tile([P, P], F32, name="ident")
         make_identity(nc, ident[:])
@@ -70,7 +68,7 @@ def tile_selfattentionlayer_pa_kernel(tc, q, k, x, Wv, bv, out):
         nc.sync.dma_start(out=bias_row[0:1, :], in_=bv.rearrange("(o d) -> o d", o=1))
 
         def transpose_pair(block_a, block_b):
-            bank = tr_banks.tile([P, 2, 2, P], F32, tag="tr", name="tr_bank")
+            bank = acc_banks.tile([P, 2, 2, P], F32, tag="acc", name="tr_bank")
             for b, block in enumerate((block_a, block_b)):
                 words = block.bitcast(F32)
                 for u in range(2):
@@ -116,7 +114,7 @@ def tile_selfattentionlayer_pa_kernel(tc, q, k, x, Wv, bv, out):
 
         on_scalar, on_vector = nc.scalar.copy, nc.vector.tensor_copy
 
-        s_banks, turn_scale, turn_bias, mean_var, halves, turns, shifted, neg_frac = {}, {}, {}, {}, {}, {}, {}, {}
+        s_banks, turn_scale, turn_bias, mean_var, halves, turns, whole, unbiased, sine_bias = {}, {}, {}, {}, {}, {}, {}, {}, {}
 
         def scores(i):
             queries = slice(i * P, (i + 1) * P)
@@ -147,7 +145,7 @@ def tile_selfattentionlayer_pa_kernel(tc, q, k, x, Wv, bv, out):
 
         def turn_factors(i):
             scaled_var = small.tile([P, 1], F32, name="scaled_var")
-            nc.gpsimd.tensor_scalar(
+            nc.vector.tensor_scalar(
                 out=scaled_var[:],
                 in0=mean_var[i][:, 1:2],
                 scalar1=TWO_PI * TWO_PI * ROWS / (ROWS - 1),
@@ -158,11 +156,20 @@ def tile_selfattentionlayer_pa_kernel(tc, q, k, x, Wv, bv, out):
             turn_scale[i] = small.tile([P, 1], F32, name="turn_scale")
             nc.gpsimd.tensor_tensor(out=turn_scale[i][:], in0=scaled_var[:], in1=neg_half[:], op=ALU.pow)
             turn_bias[i] = small.tile([P, 1], F32, name="turn_bias")
-            nc.gpsimd.tensor_scalar(
+            nc.vector.tensor_scalar(
                 out=turn_bias[i][:],
                 in0=mean_var[i][:, 0:1],
                 scalar1=turn_scale[i][:, 0:1],
                 scalar2=-1.0,
+                op0=ALU.mult,
+                op1=ALU.mult,
+            )
+            sine_bias[i] = small.tile([P, 1], F32, name="sine_bias")
+            nc.vector.tensor_scalar(
+                out=sine_bias[i][:],
+                in0=mean_var[i][:, 0:1],
+                scalar1=turn_scale[i][:, 0:1],
+                scalar2=-TWO_PI,
                 op0=ALU.mult,
                 op1=ALU.mult,
             )
@@ -179,24 +186,33 @@ def tile_selfattentionlayer_pa_kernel(tc, q, k, x, Wv, bv, out):
                 )
 
         def shift(i):
-            shifted[i] = angles.tile([P, ROWS], F32, name="shifted")
+            whole[i] = angles.tile([P, ROWS], F32, name="whole")
             nc.gpsimd.tensor_scalar(
-                out=shifted[i][:], in0=turns[i][:], scalar1=1.0, scalar2=ROUND_MAGIC, op0=ALU.mult, op1=ALU.add
-            )
-
-        def fraction(i):
-            neg_frac[i] = angles.tile([P, ROWS], F32, name="neg_frac")
-            nc.vector.scalar_tensor_tensor(
-                out=neg_frac[i][:],
-                in0=shifted[i][:],
-                scalar=ROUND_MAGIC,
-                in1=turns[i][:],
-                op0=ALU.subtract,
+                out=whole[i][:],
+                in0=turns[i][:],
+                scalar1=ROUND_MAGIC,
+                scalar2=ROUND_MAGIC,
+                op0=ALU.add,
                 op1=ALU.subtract,
             )
 
+        def fraction(i):
+            unbiased[i] = angles.tile([P, ROWS], F32, name="unbiased")
+            for h in range(2):
+                keys = slice(h * 512, (h + 1) * 512)
+                nc.vector.scalar_tensor_tensor(
+                    out=unbiased[i][:, keys],
+                    in0=s_banks[i][h][:],
+                    scalar=turn_scale[i][:, 0:1],
+                    in1=whole[i][:, keys],
+                    op0=ALU.mult,
+                    op1=ALU.subtract,
+                )
+
         def sine(i):
-            nc.scalar.activation(out=sines[:, i, :], in_=neg_frac[i][:], func=ACT.Sin, scale=-TWO_PI)
+            nc.scalar.activation(
+                out=sines[:, i, :], in_=unbiased[i][:], func=ACT.Sin, scale=TWO_PI, bias=sine_bias[i][:, 0:1]
+            )
 
         v_banks = {}
 

@@ -6,6 +6,7 @@ from concourse.masks import make_identity
 
 F32 = mybir.dt.float32
 BF16 = mybir.dt.bfloat16
+I32 = mybir.dt.int32
 U32 = mybir.dt.uint32
 U8 = mybir.dt.uint8
 FP8X4 = mybir.dt.float8_e4m3fn_x4
@@ -34,8 +35,6 @@ def tile_selfattentionlayer_pa_kernel(tc, q, k, x, Wv, bv, out):
         inputs = ctx.enter_context(tc.tile_pool(name="inputs", bufs=1))
         operands = ctx.enter_context(tc.tile_pool(name="operands", bufs=1))
         grouped_pool = ctx.enter_context(tc.tile_pool(name="grouped", bufs=6))
-        angles = ctx.enter_context(tc.tile_pool(name="angles", bufs=4))
-        e_pool = ctx.enter_context(tc.tile_pool(name="e", bufs=4))
         small = ctx.enter_context(tc.tile_pool(name="small", bufs=8))
         out_pool = ctx.enter_context(tc.tile_pool(name="out", bufs=3))
         acc_banks = ctx.enter_context(tc.psum_pool(name="acc_banks", bufs=8))
@@ -186,14 +185,9 @@ def tile_selfattentionlayer_pa_kernel(tc, q, k, x, Wv, bv, out):
                 )
 
         def shift(i):
-            whole[i] = angles.tile([P, ROWS], F32, name="whole")
+            whole[i] = angles.tile([P, ROWS], I32, name="whole")
             nc.gpsimd.tensor_scalar(
-                out=whole[i][:],
-                in0=turns[i][:],
-                scalar1=ROUND_MAGIC,
-                scalar2=ROUND_MAGIC,
-                op0=ALU.add,
-                op1=ALU.subtract,
+                out=whole[i][:], in0=turns[i][:], scalar1=1.0, scalar2=0.0, op0=ALU.mult, op1=ALU.add
             )
 
         def fraction(i):
@@ -315,71 +309,74 @@ def tile_selfattentionlayer_pa_kernel(tc, q, k, x, Wv, bv, out):
         def settle():
             quantise(*pending.pop(0))
 
-        fetch("q", 0, on_scalar)
-        fetch("k", 0, on_vector)
-        settle()
-        fetch("k", 1, on_scalar)
-        settle()
-        fetch("k", 2, on_vector)
-        settle()
-        fetch("k", 3, on_scalar)
-        settle()
-        settle()
-        fetch("q", 1, on_scalar)
-        scores(0)
-        fetch("q", 2, on_scalar)
-        statistics(0)
-        settle()
-        mean_and_variance(0)
-        turn_factors(0)
-        fetch("q", 3, on_scalar)
-        scores(1)
-        fetch("w", 0, on_scalar)
-        statistics(1)
-        settle()
-        mean_and_variance(1)
-        turn_factors(1)
-        scores(2)
-        fetch("w", 1, on_scalar)
-        to_turns(0)
-        shift(0)
-        statistics(2)
-        settle()
-        mean_and_variance(2)
-        turn_factors(2)
-        fetch("x", 0, on_scalar)
-        scores(3)
-        to_turns(1)
-        settle()
+        with tc.tile_pool(name="angles", bufs=4) as angles:
+            fetch("q", 0, on_scalar)
+            fetch("k", 0, on_vector)
+            settle()
+            fetch("k", 1, on_scalar)
+            settle()
+            fetch("k", 2, on_vector)
+            settle()
+            fetch("k", 3, on_scalar)
+            settle()
+            settle()
+            fetch("q", 1, on_scalar)
+            scores(0)
+            fetch("q", 2, on_scalar)
+            statistics(0)
+            settle()
+            mean_and_variance(0)
+            turn_factors(0)
+            fetch("q", 3, on_scalar)
+            scores(1)
+            fetch("w", 0, on_scalar)
+            statistics(1)
+            settle()
+            mean_and_variance(1)
+            turn_factors(1)
+            scores(2)
+            fetch("w", 1, on_scalar)
+            to_turns(0)
+            shift(0)
+            statistics(2)
+            settle()
+            mean_and_variance(2)
+            turn_factors(2)
+            fetch("x", 0, on_scalar)
+            scores(3)
+            to_turns(1)
+            settle()
 
-        for i in range(ROW_TILES):
-            if i + 3 < ROW_TILES:
-                statistics(i + 3)
-            if i > 0:
-                sine(i - 1)
-            if i + 2 < ROW_TILES:
-                to_turns(i + 2)
-            if i + 1 < ROW_TILES:
-                shift(i + 1)
-            if i == ROW_TILES - 2:
-                row_max(0)
-            fraction(i)
-            if i + 3 < ROW_TILES:
-                mean_and_variance(i + 3)
-                turn_factors(i + 3)
-            if pending:
-                settle()
-            if i + 4 < ROW_TILES:
-                scores(i + 4)
-            if i < 3:
-                fetch("x", i + 1, on_scalar)
-            if i == 4:
-                bias_bank = acc_banks.tile([P, FEATURES], F32, tag="acc", name="bias_bank")
-                nc.tensor.matmul(out=bias_bank[:], lhsT=ones[:], rhs=bias_row[:], start=True, stop=True)
-                bias_all = const.tile([P, FEATURES], F32, name="bias_all")
-                nc.scalar.copy(out=bias_all[:], in_=bias_bank[:])
-        sine(ROW_TILES - 1)
+            for i in range(ROW_TILES):
+                if i + 3 < ROW_TILES:
+                    statistics(i + 3)
+                if i > 0:
+                    sine(i - 1)
+                if i + 2 < ROW_TILES:
+                    to_turns(i + 2)
+                if i + 1 < ROW_TILES:
+                    shift(i + 1)
+                if i == ROW_TILES - 2:
+                    row_max(0)
+                fraction(i)
+                if i + 3 < ROW_TILES:
+                    mean_and_variance(i + 3)
+                    turn_factors(i + 3)
+                if pending:
+                    settle()
+                if i + 4 < ROW_TILES:
+                    scores(i + 4)
+                if i < 3:
+                    fetch("x", i + 1, on_scalar)
+                if i == 4:
+                    bias_bank = acc_banks.tile([P, FEATURES], F32, tag="acc", name="bias_bank")
+                    nc.tensor.matmul(out=bias_bank[:], lhsT=ones[:], rhs=bias_row[:], start=True, stop=True)
+                    bias_all = const.tile([P, FEATURES], F32, name="bias_all")
+                    nc.scalar.copy(out=bias_all[:], in_=bias_bank[:])
+            sine(ROW_TILES - 1)
 
+
+        e_pool = ctx.enter_context(tc.tile_pool(name="e", bufs=4))
         row_max(1)
         for b in range(4):
             v_products(b)
@@ -389,7 +386,7 @@ def tile_selfattentionlayer_pa_kernel(tc, q, k, x, Wv, bv, out):
         row_max(2)
         v_quantise(0)
 
-        for j in range(ROW_TILES + 1 + 1):
+        for j in range(ROW_TILES + 2 + 1):
             if j < ROW_TILES:
                 exponential(j)
                 e_banks[j] = transpose_pair(e_rows[j][:, 0:512], e_rows[j][:, 512:1024])
@@ -401,10 +398,10 @@ def tile_selfattentionlayer_pa_kernel(tc, q, k, x, Wv, bv, out):
             if j == 1:
                 v_quantise(1)
             if 1 <= j <= ROW_TILES:
-                e_grouped[j - 1] = group_words(on_vector if j - 1 in (4, 5, 6, 7) else on_scalar, e_banks[j - 1])
+                e_grouped[j - 1] = group_words(on_vector if j - 1 in (1, 3, 5, 7) else on_scalar, e_banks[j - 1])
                 invert_sum(j - 1)
-            if 1 <= j < ROW_TILES + 1:
-                e_quantise(j - 1)
-                e_times_v(j - 1)
-            if j >= 1 + 1:
-                finish(j - 1 - 1, j - 1 - 1 in (0, 2, 4, 6))
+            if 2 <= j < ROW_TILES + 2:
+                e_quantise(j - 2)
+                e_times_v(j - 2)
+            if j >= 2 + 1:
+                finish(j - 2 - 1, j - 2 - 1 in (0, 2, 4, 6))

@@ -21,6 +21,7 @@ FEATURES = 512
 ROW_TILES = ROWS // P
 KEY_PASSES = ROWS // (P * PACK)
 EPS = 1e-5
+GROUP = 4
 FLOPS = 2 * ROWS * FEATURES * FEATURES + 2 * 2 * ROWS * ROWS * FEATURES
 
 TWO_PI = 2.0 * math.pi
@@ -35,8 +36,9 @@ def tile_selfattentionlayer_pa_kernel(tc, q, k, x, Wv, bv, out):
         inputs = ctx.enter_context(tc.tile_pool(name="inputs", bufs=1))
         operands = ctx.enter_context(tc.tile_pool(name="operands", bufs=1))
         grouped_pool = ctx.enter_context(tc.tile_pool(name="grouped", bufs=6))
+        raw_pool = ctx.enter_context(tc.tile_pool(name="raw", bufs=8))
         small = ctx.enter_context(tc.tile_pool(name="small", bufs=8))
-        out_pool = ctx.enter_context(tc.tile_pool(name="out", bufs=3))
+        out_pool = ctx.enter_context(tc.tile_pool(name="out", bufs=8))
         acc_banks = ctx.enter_context(tc.psum_pool(name="acc_banks", bufs=8))
 
         ident = const.tile([P, P], F32, name="ident")
@@ -45,10 +47,10 @@ def tile_selfattentionlayer_pa_kernel(tc, q, k, x, Wv, bv, out):
         nc.vector.memset(ones[:], 1.0)
         bias_row = const.tile([P, FEATURES], BF16, name="bias_row")
         nc.vector.memset(bias_row[:], 0.0)
-        neg_half = const.tile([P, 1], F32, name="neg_half")
+        neg_half = const.tile([P, GROUP], F32, name="neg_half")
         nc.vector.memset(neg_half[:], -0.5)
         warm = const.tile([P, 1], F32, name="warm")
-        nc.scalar.activation(out=warm[:], in_=neg_half[:], func=ACT.Sin)
+        nc.scalar.activation(out=warm[:], in_=neg_half[:, 0:1], func=ACT.Sin)
 
         k_sb = inputs.tile([P, ROW_TILES, FEATURES], BF16, name="k_sb")
         q_sb = inputs.tile([P, ROW_TILES, FEATURES], BF16, name="q_sb")
@@ -113,7 +115,7 @@ def tile_selfattentionlayer_pa_kernel(tc, q, k, x, Wv, bv, out):
 
         on_scalar, on_vector = nc.scalar.copy, nc.vector.tensor_copy
 
-        s_banks, turn_scale, turn_bias, mean_var, halves, turns, whole, unbiased, sine_bias = {}, {}, {}, {}, {}, {}, {}, {}, {}
+        s_banks, turn_scale, turn_bias, mean_var, halves, raw, whole, unbiased, sine_bias = {}, {}, {}, {}, {}, {}, {}, {}, {}
 
         def scores(i):
             queries = slice(i * P, (i + 1) * P)
@@ -132,80 +134,74 @@ def tile_selfattentionlayer_pa_kernel(tc, q, k, x, Wv, bv, out):
                 )
                 s_banks[i].append(bank)
 
-        def statistics(i):
-            stats = small.tile([P, 2, 6], F32, name="stats")
-            for h in range(2):
-                nc.vector.bn_stats(out=stats[:, h, :], in_=s_banks[i][h][:])
-            halves[i] = stats
+        def statistics(i, h):
+            if h == 0:
+                halves[i] = small.tile([P, 2, 6], F32, name="stats")
+            nc.vector.bn_stats(out=halves[i][:, h, :], in_=s_banks[i][h][:])
 
         def mean_and_variance(i):
-            mean_var[i] = small.tile([P, 2], F32, name="mean_var")
-            nc.vector.bn_aggr(out=mean_var[i][:], in_=halves[i][:].rearrange("p h s -> p (h s)"))
+            g, t = divmod(i, GROUP)
+            if t == 0:
+                mean_var[g] = small.tile([P, GROUP, 2], F32, name="mean_var")
+            nc.vector.bn_aggr(out=mean_var[g][:, t, :], in_=halves[i][:].rearrange("p h s -> p (h s)"))
 
-        def turn_factors(i):
-            scaled_var = small.tile([P, 1], F32, name="scaled_var")
+        def turn_factors(g):
+            scaled_var = small.tile([P, GROUP], F32, name="scaled_var")
             nc.vector.tensor_scalar(
                 out=scaled_var[:],
-                in0=mean_var[i][:, 1:2],
+                in0=mean_var[g][:, :, 1],
                 scalar1=TWO_PI * TWO_PI * ROWS / (ROWS - 1),
                 scalar2=TWO_PI * TWO_PI * EPS,
                 op0=ALU.mult,
                 op1=ALU.add,
             )
-            turn_scale[i] = small.tile([P, 1], F32, name="turn_scale")
-            nc.gpsimd.tensor_tensor(out=turn_scale[i][:], in0=scaled_var[:], in1=neg_half[:], op=ALU.pow)
-            turn_bias[i] = small.tile([P, 1], F32, name="turn_bias")
-            nc.vector.tensor_scalar(
-                out=turn_bias[i][:],
-                in0=mean_var[i][:, 0:1],
-                scalar1=turn_scale[i][:, 0:1],
-                scalar2=-1.0,
+            turn_scale[g] = small.tile([P, GROUP], F32, name="turn_scale")
+            nc.gpsimd.tensor_tensor(out=turn_scale[g][:], in0=scaled_var[:], in1=neg_half[:], op=ALU.pow)
+            turn_bias[g] = small.tile([P, GROUP], F32, name="turn_bias")
+            nc.vector.scalar_tensor_tensor(
+                out=turn_bias[g][:],
+                in0=mean_var[g][:, :, 0],
+                scalar=-1.0,
+                in1=turn_scale[g][:],
                 op0=ALU.mult,
                 op1=ALU.mult,
             )
-            sine_bias[i] = small.tile([P, 1], F32, name="sine_bias")
+            sine_bias[g] = small.tile([P, GROUP], F32, name="sine_bias")
             nc.vector.tensor_scalar(
-                out=sine_bias[i][:],
-                in0=mean_var[i][:, 0:1],
-                scalar1=turn_scale[i][:, 0:1],
-                scalar2=-TWO_PI,
-                op0=ALU.mult,
-                op1=ALU.mult,
+                out=sine_bias[g][:], in0=turn_bias[g][:], scalar1=TWO_PI, scalar2=None, op0=ALU.mult
             )
 
-        def to_turns(i):
-            turns[i] = angles.tile([P, ROWS], F32, name="turns")
+        def of_tile(factor, i):
+            g, t = divmod(i, GROUP)
+            return factor[g][:, t : t + 1]
+
+        def copy_scores(i):
+            raw[i] = raw_pool.tile([P, ROWS], F32, name="raw")
             for h in range(2):
-                nc.scalar.activation(
-                    out=turns[i][:, h * 512 : (h + 1) * 512],
-                    in_=s_banks[i][h][:],
-                    func=ACT.Identity,
-                    bias=turn_bias[i][:, 0:1],
-                    scale=turn_scale[i][:, 0:1],
-                )
+                nc.scalar.copy(out=raw[i][:, h * 512 : (h + 1) * 512], in_=s_banks[i][h][:])
 
         def shift(i):
             whole[i] = angles.tile([P, ROWS], I32, name="whole")
             nc.gpsimd.tensor_scalar(
-                out=whole[i][:], in0=turns[i][:], scalar1=1.0, scalar2=0.0, op0=ALU.mult, op1=ALU.add
+                out=whole[i][:], in0=raw[i][:], scalar1=of_tile(turn_scale, i), scalar2=of_tile(turn_bias, i), op0=ALU.mult, op1=ALU.add
             )
 
-        def fraction(i):
-            unbiased[i] = angles.tile([P, ROWS], F32, name="unbiased")
-            for h in range(2):
-                keys = slice(h * 512, (h + 1) * 512)
-                nc.vector.scalar_tensor_tensor(
-                    out=unbiased[i][:, keys],
-                    in0=s_banks[i][h][:],
-                    scalar=turn_scale[i][:, 0:1],
-                    in1=whole[i][:, keys],
-                    op0=ALU.mult,
-                    op1=ALU.subtract,
-                )
+        def fraction(i, h):
+            if h == 0:
+                unbiased[i] = angles.tile([P, ROWS], F32, name="unbiased")
+            keys = slice(h * 512, (h + 1) * 512)
+            nc.vector.scalar_tensor_tensor(
+                out=unbiased[i][:, keys],
+                in0=s_banks[i][h][:],
+                scalar=of_tile(turn_scale, i),
+                in1=whole[i][:, keys],
+                op0=ALU.mult,
+                op1=ALU.subtract,
+            )
 
         def sine(i):
             nc.scalar.activation(
-                out=sines[:, i, :], in_=unbiased[i][:], func=ACT.Sin, scale=TWO_PI, bias=sine_bias[i][:, 0:1]
+                out=sines[:, i, :], in_=unbiased[i][:], func=ACT.Sin, scale=TWO_PI, bias=of_tile(sine_bias, i)
             )
 
         v_banks = {}
@@ -320,88 +316,55 @@ def tile_selfattentionlayer_pa_kernel(tc, q, k, x, Wv, bv, out):
             fetch("k", 3, on_scalar)
             settle()
             settle()
-            fetch("q", 1, on_scalar)
-            scores(0)
-            fetch("q", 2, on_scalar)
-            statistics(0)
-            settle()
-            mean_and_variance(0)
-            turn_factors(0)
-            fetch("q", 3, on_scalar)
-            scores(1)
-            fetch("w", 0, on_scalar)
-            statistics(1)
-            settle()
-            mean_and_variance(1)
-            turn_factors(1)
-            scores(2)
-            fetch("w", 1, on_scalar)
-            to_turns(0)
-            shift(0)
-            statistics(2)
-            settle()
-            mean_and_variance(2)
-            turn_factors(2)
-            fetch("x", 0, on_scalar)
-            scores(3)
-            to_turns(1)
-            settle()
-
             for i in range(ROW_TILES):
-                if i + 3 < ROW_TILES:
-                    statistics(i + 3)
-                if i > 0:
-                    sine(i - 1)
-                if i + 2 < ROW_TILES:
-                    to_turns(i + 2)
-                if i + 1 < ROW_TILES:
-                    shift(i + 1)
-                if i == ROW_TILES - 2:
-                    row_max(0)
-                fraction(i)
-                if i + 3 < ROW_TILES:
-                    mean_and_variance(i + 3)
-                    turn_factors(i + 3)
-                if pending:
+                if i in (0, 2, 4):
+                    fetch("q", i // 2 + 1, on_scalar)
+                scores(i)
+                copy_scores(i)
+                statistics(i, 0)
+                statistics(i, 1)
+                mean_and_variance(i)
+                if i in (0, 2, 4):
                     settle()
-                if i + 4 < ROW_TILES:
-                    scores(i + 4)
-                if i < 3:
-                    fetch("x", i + 1, on_scalar)
-                if i == 4:
-                    bias_bank = acc_banks.tile([P, FEATURES], F32, tag="acc", name="bias_bank")
-                    nc.tensor.matmul(out=bias_bank[:], lhsT=ones[:], rhs=bias_row[:], start=True, stop=True)
-                    bias_all = const.tile([P, FEATURES], F32, name="bias_all")
-                    nc.scalar.copy(out=bias_all[:], in_=bias_bank[:])
-            sine(ROW_TILES - 1)
+                if i % GROUP == GROUP - 1:
+                    turn_factors(i // GROUP)
+            for i in range(ROW_TILES):
+                shift(i)
+                scores(i)
+                fraction(i, 0)
+                fraction(i, 1)
+                sine(i)
+                if i < 6:
+                    fetch(*(("w", i) if i < 2 else ("x", i - 2)), on_scalar)
+                    settle()
 
 
         e_pool = ctx.enter_context(tc.tile_pool(name="e", bufs=4))
-        row_max(1)
+        bias_bank = acc_banks.tile([P, FEATURES], F32, tag="acc", name="bias_bank")
+        nc.tensor.matmul(out=bias_bank[:], lhsT=ones[:], rhs=bias_row[:], start=True, stop=True)
+        bias_all = const.tile([P, FEATURES], F32, name="bias_all")
+        nc.scalar.copy(out=bias_all[:], in_=bias_bank[:])
         for b in range(4):
             v_products(b)
-        for b in range(4):
-            v_add(b)
-            v_products(b + 4)
-        row_max(2)
-        v_quantise(0)
-
-        for j in range(ROW_TILES + 2 + 1):
+        for j in range(2):
+            row_max(j)
+        for j in range(ROW_TILES + 3 + 1):
             if j < ROW_TILES:
                 exponential(j)
                 e_banks[j] = transpose_pair(e_rows[j][:, 0:512], e_rows[j][:, 512:1024])
-            if j in (0, 1):
-                v_add(2 * j + 4)
-                v_add(2 * j + 5)
-            if j + 3 < ROW_TILES:
-                row_max(j + 3)
-            if j == 1:
-                v_quantise(1)
+            if j + 2 < ROW_TILES:
+                row_max(j + 2)
+            for b in range(2 * j, min(2 * j + 2, 8)):
+                v_add(b)
+                if b < 4:
+                    v_products(b + 4)
+                if b % 4 == 3:
+                    v_quantise(b // 4)
             if 1 <= j <= ROW_TILES:
-                e_grouped[j - 1] = group_words(on_vector if j - 1 in (1, 3, 5, 7) else on_scalar, e_banks[j - 1])
+                e_grouped[j - 1] = group_words(on_vector if j - 1 in (6, 7) else on_scalar, e_banks[j - 1])
                 invert_sum(j - 1)
-            if 2 <= j < ROW_TILES + 2:
-                e_quantise(j - 2)
-                e_times_v(j - 2)
-            if j >= 2 + 1:
-                finish(j - 2 - 1, j - 2 - 1 in (0, 2, 4, 6))
+            if 3 <= j < ROW_TILES + 3:
+                e_quantise(j - 3)
+                e_times_v(j - 3)
+            if j >= 3 + 1:
+                finish(j - 3 - 1, j - 3 - 1 in (0, 1, 2))

@@ -117,27 +117,24 @@ def tile_selfattentionlayer_pa_kernel(tc, q, k, x, Wv, bv, out):
 
         s_banks, turn_scale, turn_bias, mean_var, halves, raw, whole, unbiased, sine_bias = {}, {}, {}, {}, {}, {}, {}, {}, {}
 
-        def scores(i):
+        def scores(i, h):
             queries = slice(i * P, (i + 1) * P)
-            s_banks[i] = []
-            for h in range(2):
-                keys = slice(h * 512, (h + 1) * 512)
-                bank = acc_banks.tile([P, FEATURES], F32, tag="acc", name="s_bank")
-                nc.tensor.matmul_mx(
-                    out=bank[:],
-                    lhsT=q_codes[:, queries].bitcast(FP8X4),
-                    lhsT_scale=q_scales[:, queries],
-                    rhs=k_codes[:, keys].bitcast(FP8X4),
-                    rhs_scale=k_scales[:, keys],
-                    start=True,
-                    stop=True,
-                )
-                s_banks[i].append(bank)
+            keys = slice(h * 512, (h + 1) * 512)
+            s_banks[i, h] = acc_banks.tile([P, FEATURES], F32, tag="acc", name="s_bank")
+            nc.tensor.matmul_mx(
+                out=s_banks[i, h][:],
+                lhsT=q_codes[:, queries].bitcast(FP8X4),
+                lhsT_scale=q_scales[:, queries],
+                rhs=k_codes[:, keys].bitcast(FP8X4),
+                rhs_scale=k_scales[:, keys],
+                start=True,
+                stop=True,
+            )
 
         def statistics(i, h):
             if h == 0:
                 halves[i] = small.tile([P, 2, 6], F32, name="stats")
-            nc.vector.bn_stats(out=halves[i][:, h, :], in_=s_banks[i][h][:])
+            nc.vector.bn_stats(out=halves[i][:, h, :], in_=s_banks[i, h][:])
 
         def mean_and_variance(i):
             g, t = divmod(i, GROUP)
@@ -157,6 +154,8 @@ def tile_selfattentionlayer_pa_kernel(tc, q, k, x, Wv, bv, out):
             )
             turn_scale[g] = small.tile([P, GROUP], F32, name="turn_scale")
             nc.gpsimd.tensor_tensor(out=turn_scale[g][:], in0=scaled_var[:], in1=neg_half[:], op=ALU.pow)
+
+        def biases(g):
             turn_bias[g] = small.tile([P, GROUP], F32, name="turn_bias")
             nc.vector.scalar_tensor_tensor(
                 out=turn_bias[g][:],
@@ -175,10 +174,10 @@ def tile_selfattentionlayer_pa_kernel(tc, q, k, x, Wv, bv, out):
             g, t = divmod(i, GROUP)
             return factor[g][:, t : t + 1]
 
-        def copy_scores(i):
-            raw[i] = raw_pool.tile([P, ROWS], F32, name="raw")
-            for h in range(2):
-                nc.scalar.copy(out=raw[i][:, h * 512 : (h + 1) * 512], in_=s_banks[i][h][:])
+        def copy_scores(i, h):
+            if h == 0:
+                raw[i] = raw_pool.tile([P, ROWS], F32, name="raw")
+            nc.scalar.copy(out=raw[i][:, h * 512 : (h + 1) * 512], in_=s_banks[i, h][:])
 
         def shift(i):
             whole[i] = angles.tile([P, ROWS], I32, name="whole")
@@ -192,7 +191,7 @@ def tile_selfattentionlayer_pa_kernel(tc, q, k, x, Wv, bv, out):
             keys = slice(h * 512, (h + 1) * 512)
             nc.vector.scalar_tensor_tensor(
                 out=unbiased[i][:, keys],
-                in0=s_banks[i][h][:],
+                in0=s_banks[i, h][:],
                 scalar=of_tile(turn_scale, i),
                 in1=whole[i][:, keys],
                 op0=ALU.mult,
@@ -307,11 +306,11 @@ def tile_selfattentionlayer_pa_kernel(tc, q, k, x, Wv, bv, out):
 
         with tc.tile_pool(name="angles", bufs=4) as angles:
             fetch("q", 0, on_scalar)
-            fetch("k", 0, on_vector)
+            fetch("k", 0, on_scalar)
             settle()
             fetch("k", 1, on_scalar)
             settle()
-            fetch("k", 2, on_vector)
+            fetch("k", 2, on_scalar)
             settle()
             fetch("k", 3, on_scalar)
             settle()
@@ -319,21 +318,25 @@ def tile_selfattentionlayer_pa_kernel(tc, q, k, x, Wv, bv, out):
             for i in range(ROW_TILES):
                 if i in (0, 2, 4):
                     fetch("q", i // 2 + 1, on_scalar)
-                scores(i)
-                copy_scores(i)
-                statistics(i, 0)
-                statistics(i, 1)
+                for h in range(2):
+                    scores(i, h)
+                    statistics(i, h)
+                    copy_scores(i, h)
                 mean_and_variance(i)
                 if i in (0, 2, 4):
                     settle()
                 if i % GROUP == GROUP - 1:
                     turn_factors(i // GROUP)
+                if i == GROUP + 1:
+                    biases(0)
             for i in range(ROW_TILES):
                 shift(i)
-                scores(i)
-                fraction(i, 0)
-                fraction(i, 1)
+                for h in range(2):
+                    scores(i, h)
+                    fraction(i, h)
                 sine(i)
+                if i == 3:
+                    biases(1)
                 if i < 6:
                     fetch(*(("w", i) if i < 2 else ("x", i - 2)), on_scalar)
                     settle()
@@ -346,14 +349,14 @@ def tile_selfattentionlayer_pa_kernel(tc, q, k, x, Wv, bv, out):
         nc.scalar.copy(out=bias_all[:], in_=bias_bank[:])
         for b in range(4):
             v_products(b)
-        for j in range(2):
+        for j in range(3):
             row_max(j)
         for j in range(ROW_TILES + 3 + 1):
             if j < ROW_TILES:
                 exponential(j)
                 e_banks[j] = transpose_pair(e_rows[j][:, 0:512], e_rows[j][:, 512:1024])
-            if j + 2 < ROW_TILES:
-                row_max(j + 2)
+            if j + 3 < ROW_TILES:
+                row_max(j + 3)
             for b in range(2 * j, min(2 * j + 2, 8)):
                 v_add(b)
                 if b < 4:

@@ -43,10 +43,6 @@ def tile_selfattentionlayer_pa_kernel(tc, q, k, x, Wv, bv, out):
 
         ident = const.tile([P, P], F32, name="ident")
         make_identity(nc, ident[:])
-        ones = const.tile([P, P], BF16, name="ones")
-        nc.vector.memset(ones[:], 1.0)
-        bias_row = const.tile([P, FEATURES], BF16, name="bias_row")
-        nc.vector.memset(bias_row[:], 0.0)
         neg_half = const.tile([P, GROUP], F32, name="neg_half")
         nc.vector.memset(neg_half[:], -0.5)
         warm = const.tile([P, 1], F32, name="warm")
@@ -66,7 +62,8 @@ def tile_selfattentionlayer_pa_kernel(tc, q, k, x, Wv, bv, out):
             nc.sync.dma_start(
                 out=x_sb[:, c, :, :], in_=x[c * 256 : (c + 1) * 256, :].rearrange("(p e) d -> p e d", e=2)
             )
-        nc.sync.dma_start(out=bias_row[0:1, :], in_=bv.rearrange("(o d) -> o d", o=1))
+        bias_all = inputs.tile([P, FEATURES], BF16, name="bias_all")
+        nc.sync.dma_start(out=bias_all[:], in_=bv.partition_broadcast(P))
 
         def transpose_pair(block_a, block_b):
             bank = acc_banks.tile([P, 2, 2, P], F32, tag="acc", name="tr_bank")
@@ -115,7 +112,7 @@ def tile_selfattentionlayer_pa_kernel(tc, q, k, x, Wv, bv, out):
 
         on_scalar, on_vector = nc.scalar.copy, nc.vector.tensor_copy
 
-        s_banks, turn_scale, turn_bias, mean_var, halves, raw, whole, unbiased, sine_bias = {}, {}, {}, {}, {}, {}, {}, {}, {}
+        s_banks, turn_scale, turn_bias, mean_var, minus_mean, halves, raw, whole, unbiased, sine_bias = {}, {}, {}, {}, {}, {}, {}, {}, {}, {}
 
         def scores(i, h):
             queries = slice(i * P, (i + 1) * P)
@@ -144,31 +141,27 @@ def tile_selfattentionlayer_pa_kernel(tc, q, k, x, Wv, bv, out):
 
         def turn_factors(g):
             scaled_var = small.tile([P, GROUP], F32, name="scaled_var")
-            nc.vector.tensor_scalar(
+            nc.scalar.activation(
                 out=scaled_var[:],
-                in0=mean_var[g][:, :, 1],
-                scalar1=TWO_PI * TWO_PI * ROWS / (ROWS - 1),
-                scalar2=TWO_PI * TWO_PI * EPS,
-                op0=ALU.mult,
-                op1=ALU.add,
+                in_=mean_var[g][:, :, 1],
+                func=ACT.Copy,
+                scale=TWO_PI * TWO_PI * ROWS / (ROWS - 1),
+                bias=TWO_PI * TWO_PI * EPS,
             )
+            minus_mean[g] = small.tile([P, GROUP], F32, name="minus_mean")
+            nc.scalar.mul(out=minus_mean[g][:], in_=mean_var[g][:, :, 0], mul=-1.0)
             turn_scale[g] = small.tile([P, GROUP], F32, name="turn_scale")
             nc.gpsimd.tensor_tensor(out=turn_scale[g][:], in0=scaled_var[:], in1=neg_half[:], op=ALU.pow)
 
         def biases(g):
             turn_bias[g] = small.tile([P, GROUP], F32, name="turn_bias")
-            nc.vector.scalar_tensor_tensor(
-                out=turn_bias[g][:],
-                in0=mean_var[g][:, :, 0],
-                scalar=-1.0,
-                in1=turn_scale[g][:],
-                op0=ALU.mult,
-                op1=ALU.mult,
+            nc.gpsimd.tensor_tensor(
+                out=turn_bias[g][:], in0=minus_mean[g][:], in1=turn_scale[g][:], op=ALU.mult
             )
+
+        def sine_factor(g):
             sine_bias[g] = small.tile([P, GROUP], F32, name="sine_bias")
-            nc.vector.tensor_scalar(
-                out=sine_bias[g][:], in0=turn_bias[g][:], scalar1=TWO_PI, scalar2=None, op0=ALU.mult
-            )
+            nc.scalar.mul(out=sine_bias[g][:], in_=turn_bias[g][:], mul=TWO_PI)
 
         def of_tile(factor, i):
             g, t = divmod(i, GROUP)
@@ -250,19 +243,21 @@ def tile_selfattentionlayer_pa_kernel(tc, q, k, x, Wv, bv, out):
 
         def exponential(i):
             e_rows[i] = e_pool.tile([P, ROWS], BF16, name="e_rows")
-            row_sum[i] = small.tile([P, 1], F32, name="row_sum")
+            pair, t = divmod(i, 2)
+            if t == 0:
+                row_sum[pair] = small.tile([P, 2], F32, name="row_sum")
             nc.scalar.activation(
                 out=e_rows[i][:],
                 in_=sines[:, i, :],
                 func=ACT.Exp,
                 bias=exp_bias[i][:, 0:1],
                 scale=INV_SQRT_FEATURES,
-                accum_out=row_sum[i][:, 0:1],
+                accum_out=row_sum[pair][:, t : t + 1],
             )
 
-        def invert_sum(i):
-            inv_sum[i] = small.tile([P, 1], F32, name="inv_sum")
-            nc.vector.reciprocal(out=inv_sum[i][:], in_=row_sum[i][:])
+        def invert_sums(pair):
+            inv_sum[pair] = small.tile([P, 2], F32, name="inv_sum")
+            nc.vector.reciprocal(out=inv_sum[pair][:], in_=row_sum[pair][:])
 
         def e_quantise(i):
             codes = e_pool.tile([P, KEY_PASSES * P], U32, align_bytes=64, name="e_codes")
@@ -286,13 +281,15 @@ def tile_selfattentionlayer_pa_kernel(tc, q, k, x, Wv, bv, out):
                 )
 
         def finish(i, on_vec):
+            pair, t = divmod(i, 2)
+            inverse = inv_sum[pair][:, t : t + 1]
             result = out_pool.tile([P, FEATURES], F32, name="result")
             if on_vec:
                 nc.vector.tensor_scalar(
-                    out=result[:], in0=out_banks[i][:], scalar1=inv_sum[i][:, 0:1], scalar2=None, op0=ALU.mult
+                    out=result[:], in0=out_banks[i][:], scalar1=inverse, scalar2=None, op0=ALU.mult
                 )
             else:
-                nc.scalar.activation(out=result[:], in_=out_banks[i][:], func=ACT.Copy, scale=inv_sum[i][:, 0:1])
+                nc.scalar.activation(out=result[:], in_=out_banks[i][:], func=ACT.Copy, scale=inverse)
             nc.sync.dma_start(out=out[i * P : (i + 1) * P, :], in_=result[:])
 
         pending = []
@@ -327,29 +324,28 @@ def tile_selfattentionlayer_pa_kernel(tc, q, k, x, Wv, bv, out):
                     settle()
                 if i % GROUP == GROUP - 1:
                     turn_factors(i // GROUP)
-                if i == GROUP + 1:
+                if i == GROUP + 0:
                     biases(0)
+            biases(1)
             for i in range(ROW_TILES):
                 shift(i)
                 for h in range(2):
                     scores(i, h)
                     fraction(i, h)
+                if i % GROUP == 0:
+                    sine_factor(i // GROUP)
                 sine(i)
                 if i == 3:
-                    biases(1)
+                    row_max(0)
                 if i < 6:
                     fetch(*(("w", i) if i < 2 else ("x", i - 2)), on_scalar)
                     settle()
 
 
         e_pool = ctx.enter_context(tc.tile_pool(name="e", bufs=4))
-        bias_bank = acc_banks.tile([P, FEATURES], F32, tag="acc", name="bias_bank")
-        nc.tensor.matmul(out=bias_bank[:], lhsT=ones[:], rhs=bias_row[:], start=True, stop=True)
-        bias_all = const.tile([P, FEATURES], F32, name="bias_all")
-        nc.scalar.copy(out=bias_all[:], in_=bias_bank[:])
         for b in range(4):
             v_products(b)
-        for j in range(3):
+        for j in range(1, 3):
             row_max(j)
         for j in range(ROW_TILES + 3 + 1):
             if j < ROW_TILES:
@@ -365,7 +361,8 @@ def tile_selfattentionlayer_pa_kernel(tc, q, k, x, Wv, bv, out):
                     v_quantise(b // 4)
             if 1 <= j <= ROW_TILES:
                 e_grouped[j - 1] = group_words(on_vector if j - 1 in (6, 7) else on_scalar, e_banks[j - 1])
-                invert_sum(j - 1)
+                if j % 2 == 0:
+                    invert_sums(j // 2 - 1)
             if 3 <= j < ROW_TILES + 3:
                 e_quantise(j - 3)
                 e_times_v(j - 3)

@@ -37,6 +37,7 @@ def tile_selfattentionlayer_pa_kernel(tc, q, k, x, Wv, bv, out):
         operands = ctx.enter_context(tc.tile_pool(name="operands", bufs=1))
         grouped_pool = ctx.enter_context(tc.tile_pool(name="grouped", bufs=6))
         raw_pool = ctx.enter_context(tc.tile_pool(name="raw", bufs=8))
+        wide_pool = ctx.enter_context(tc.tile_pool(name="wide", bufs=3))
         small = ctx.enter_context(tc.tile_pool(name="small", bufs=8))
         out_pool = ctx.enter_context(tc.tile_pool(name="out", bufs=8))
         acc_banks = ctx.enter_context(tc.psum_pool(name="acc_banks", bufs=8))
@@ -47,6 +48,12 @@ def tile_selfattentionlayer_pa_kernel(tc, q, k, x, Wv, bv, out):
         nc.vector.memset(neg_half[:], -0.5)
         warm = const.tile([P, 1], F32, name="warm")
         nc.scalar.activation(out=warm[:], in_=neg_half[:, 0:1], func=ACT.Sin)
+
+        zeros = const.tile([P, FEATURES], BF16, name="zeros")
+        nc.vector.memset(zeros[:], 0.0)
+        for w in range(4):
+            nothing = acc_banks.tile([P, FEATURES], F32, tag="acc", name="nothing")
+            nc.tensor.matmul(out=nothing[:], lhsT=zeros[:, 0:P], rhs=zeros[:], start=True, stop=True)
 
         k_sb = inputs.tile([P, ROW_TILES, FEATURES], BF16, name="k_sb")
         q_sb = inputs.tile([P, ROW_TILES, FEATURES], BF16, name="q_sb")
@@ -75,8 +82,9 @@ def tile_selfattentionlayer_pa_kernel(tc, q, k, x, Wv, bv, out):
                     )
             return bank
 
-        def group_words(copy, bank):
-            grouped = grouped_pool.tile([P, 2 * P * PACK], BF16, align_bytes=64, tag="grouped", name="grouped")
+        def group_words(copy, bank, grouped=None):
+            if grouped is None:
+                grouped = grouped_pool.tile([P, 2 * P * PACK], BF16, align_bytes=64, tag="grouped", name="grouped")
             copy(
                 out=grouped[:].bitcast(F32).rearrange("p (b r u) -> p b r u", b=2, u=2),
                 in_=bank[:].rearrange("p b u r -> p b r u"),
@@ -88,8 +96,8 @@ def tile_selfattentionlayer_pa_kernel(tc, q, k, x, Wv, bv, out):
             scales = operands.tile([P, columns], U8, align_bytes=64, name=name + "_scales")
             return codes, scales
 
-        def quantise(grouped, codes, scales, c):
-            cols = slice(c * 2 * P, (c + 1) * 2 * P)
+        def quantise(grouped, codes, scales, c, width=2 * P):
+            cols = slice(c * 2 * P, c * 2 * P + width)
             nc.vector.quantize_mx(out=codes[:, cols].bitcast(FP8X4), scales=scales[:, cols], in_=grouped[:])
 
         k_codes, k_scales = new_operand(ROWS, "k")
@@ -301,6 +309,18 @@ def tile_selfattentionlayer_pa_kernel(tc, q, k, x, Wv, bv, out):
         def settle():
             quantise(*pending.pop(0))
 
+
+        wide = {}
+
+        def fetch_half(name, c):
+            block_a, block_b, codes, scales = blocks_of(name, c)
+            if c % 2 == 0:
+                wide[name] = wide_pool.tile([P, 4 * P * PACK], BF16, align_bytes=64, name="wide")
+            half = slice((c % 2) * 2 * P * PACK, (c % 2 + 1) * 2 * P * PACK)
+            group_words(on_scalar, transpose_pair(block_a, block_b), wide[name][:, half])
+            if c % 2 == 1:
+                quantise(wide[name], codes, scales, c - 1, width=4 * P)
+
         with tc.tile_pool(name="angles", bufs=4) as angles:
             fetch("q", 0, on_scalar)
             fetch("k", 0, on_scalar)
@@ -324,9 +344,7 @@ def tile_selfattentionlayer_pa_kernel(tc, q, k, x, Wv, bv, out):
                     settle()
                 if i % GROUP == GROUP - 1:
                     turn_factors(i // GROUP)
-                if i == GROUP + 0:
-                    biases(0)
-            biases(1)
+                    biases(i // GROUP)
             for i in range(ROW_TILES):
                 shift(i)
                 for h in range(2):
@@ -338,8 +356,7 @@ def tile_selfattentionlayer_pa_kernel(tc, q, k, x, Wv, bv, out):
                 if i == 3:
                     row_max(0)
                 if i < 6:
-                    fetch(*(("w", i) if i < 2 else ("x", i - 2)), on_scalar)
-                    settle()
+                    fetch_half(*(("w", i) if i < 2 else ("x", i - 2)))
 
 
         e_pool = ctx.enter_context(tc.tile_pool(name="e", bufs=4))

@@ -182,7 +182,8 @@ def tile_selfattentionlayer_pa_kernel(tc, q, k, x, Wv, bv, out):
 
         def shift(i):
             whole[i] = angles.tile([P, ROWS], I32, name="whole")
-            nc.gpsimd.tensor_scalar(
+            engine = nc.vector if i in (3,) else nc.gpsimd
+            engine.tensor_scalar(
                 out=whole[i][:], in0=raw[i][:], scalar1=of_tile(turn_scale, i), scalar2=of_tile(turn_bias, i), op0=ALU.mult, op1=ALU.add
             )
 

import math
from contextlib import ExitStack

import concourse.mybir as mybir
from concourse.masks import make_identity

F32 = mybir.dt.float32
BF16 = mybir.dt.bfloat16
I32 = mybir.dt.int32
U32 = mybir.dt.uint32
U8 = mybir.dt.uint8
FP8X4 = mybir.dt.float8_e4m3fn_x4
ALU = mybir.AluOpType
ACT = mybir.ActivationFunctionType
AXIS = mybir.AxisListType

P = 128
PACK = 4
ROWS = 1024
FEATURES = 512
ROW_TILES = ROWS // P
KEY_PASSES = ROWS // (P * PACK)
EPS = 1e-5
GROUP = 4
FLOPS = 2 * ROWS * FEATURES * FEATURES + 2 * 2 * ROWS * ROWS * FEATURES

TWO_PI = 2.0 * math.pi
INV_SQRT_FEATURES = 1.0 / math.sqrt(FEATURES)
ROUND_MAGIC = 12582912.0


def tile_selfattentionlayer_pa_kernel(tc, q, k, x, Wv, bv, out):
    nc = tc.nc
    with ExitStack() as ctx:
        const = ctx.enter_context(tc.tile_pool(name="const", bufs=1))
        inputs = ctx.enter_context(tc.tile_pool(name="inputs", bufs=1))
        operands = ctx.enter_context(tc.tile_pool(name="operands", bufs=1))
        grouped_pool = ctx.enter_context(tc.tile_pool(name="grouped", bufs=6))
        raw_pool = ctx.enter_context(tc.tile_pool(name="raw", bufs=8))
        wide_pool = ctx.enter_context(tc.tile_pool(name="wide", bufs=3))
        small = ctx.enter_context(tc.tile_pool(name="small", bufs=8))
        out_pool = ctx.enter_context(tc.tile_pool(name="out", bufs=8))
        acc_banks = ctx.enter_context(tc.psum_pool(name="acc_banks", bufs=8))

        ident = const.tile([P, P], F32, name="ident")
        make_identity(nc, ident[:])
        neg_half = const.tile([P, GROUP], F32, name="neg_half")
        nc.vector.memset(neg_half[:], -0.5)
        warm = const.tile([P, 1], F32, name="warm")
        nc.scalar.activation(out=warm[:], in_=neg_half[:, 0:1], func=ACT.Sin)

        zeros = const.tile([P, FEATURES], BF16, name="zeros")
        nc.vector.memset(zeros[:], 0.0)
        for w in range(4):
            nothing = acc_banks.tile([P, FEATURES], F32, tag="acc", name="nothing")
            nc.tensor.matmul(out=nothing[:], lhsT=zeros[:, 0:P], rhs=zeros[:], start=True, stop=True)

        k_sb = inputs.tile([P, ROW_TILES, FEATURES], BF16, name="k_sb")
        q_sb = inputs.tile([P, ROW_TILES, FEATURES], BF16, name="q_sb")
        for src, dst, c in [(q, q_sb, 0)] + [(k, k_sb, c) for c in range(4)] + [(q, q_sb, c) for c in range(1, 4)]:
            nc.sync.dma_start(
                out=dst[:, 2 * c : 2 * c + 2, :],
                in_=src[c * 256 : (c + 1) * 256, :].rearrange("(t p) d -> p t d", p=P),
            )
        wv_sb = inputs.tile([P, 4, FEATURES], BF16, name="wv_sb")
        nc.sync.dma_start(out=wv_sb[:], in_=Wv.rearrange("(t p) d -> p t d", p=P))
        x_sb = inputs.tile([P, 4, 2, FEATURES], BF16, name="x_sb")
        for c in range(4):
            nc.sync.dma_start(
                out=x_sb[:, c, :, :], in_=x[c * 256 : (c + 1) * 256, :].rearrange("(p e) d -> p e d", e=2)
            )
        bias_all = inputs.tile([P, FEATURES], BF16, name="bias_all")
        nc.sync.dma_start(out=bias_all[:], in_=bv.partition_broadcast(P))

        def transpose_pair(block_a, block_b):
            bank = acc_banks.tile([P, 2, 2, P], F32, tag="acc", name="tr_bank")
            for b, block in enumerate((block_a, block_b)):
                words = block.bitcast(F32)
                for u in range(2):
                    nc.tensor.transpose(
                        out=bank[:, b, u, :], in_=words[:, u * P : (u + 1) * P], identity=ident[:]
                    )
            return bank

        def group_words(copy, bank, grouped=None):
            if grouped is None:
                grouped = grouped_pool.tile([P, 2 * P * PACK], BF16, align_bytes=64, tag="grouped", name="grouped")
            copy(
                out=grouped[:].bitcast(F32).rearrange("p (b r u) -> p b r u", b=2, u=2),
                in_=bank[:].rearrange("p b u r -> p b r u"),
            )
            return grouped

        def new_operand(columns, name):
            codes = operands.tile([P, columns], U32, align_bytes=64, name=name + "_codes")
            scales = operands.tile([P, columns], U8, align_bytes=64, name=name + "_scales")
            return codes, scales

        def quantise(grouped, codes, scales, c, width=2 * P):
            cols = slice(c * 2 * P, c * 2 * P + width)
            nc.vector.quantize_mx(out=codes[:, cols].bitcast(FP8X4), scales=scales[:, cols], in_=grouped[:])

        k_codes, k_scales = new_operand(ROWS, "k")
        q_codes, q_scales = new_operand(ROWS, "q")
        wv_codes, wv_scales = new_operand(FEATURES, "wv")
        x_codes, x_scales = new_operand(ROWS, "x")
        sines = operands.tile([P, ROW_TILES, ROWS], F32, name="sines")
        v_grouped = operands.tile([P, KEY_PASSES, FEATURES, PACK], BF16, align_bytes=64, name="v_grouped")
        v_codes = operands.tile([P, KEY_PASSES, FEATURES], U32, align_bytes=64, name="v_codes")
        v_scales = operands.tile([P, KEY_PASSES, FEATURES], U8, align_bytes=64, name="v_scales")

        def blocks_of(name, c):
            if name == "k":
                return k_sb[:, 2 * c, :], k_sb[:, 2 * c + 1, :], k_codes, k_scales
            if name == "q":
                return q_sb[:, 2 * c, :], q_sb[:, 2 * c + 1, :], q_codes, q_scales
            if name == "w":
                return wv_sb[:, 2 * c, :], wv_sb[:, 2 * c + 1, :], wv_codes, wv_scales
            return x_sb[:, c, 0, :], x_sb[:, c, 1, :], x_codes, x_scales

        on_scalar, on_vector = nc.scalar.copy, nc.vector.tensor_copy

        s_banks, turn_scale, turn_bias, mean_var, minus_mean, halves, raw, whole, unbiased, sine_bias = {}, {}, {}, {}, {}, {}, {}, {}, {}, {}

        def scores(i, h):
            queries = slice(i * P, (i + 1) * P)
            keys = slice(h * 512, (h + 1) * 512)
            s_banks[i, h] = acc_banks.tile([P, FEATURES], F32, tag="acc", name="s_bank")
            nc.tensor.matmul_mx(
                out=s_banks[i, h][:],
                lhsT=q_codes[:, queries].bitcast(FP8X4),
                lhsT_scale=q_scales[:, queries],
                rhs=k_codes[:, keys].bitcast(FP8X4),
                rhs_scale=k_scales[:, keys],
                start=True,
                stop=True,
            )

        def statistics(i, h):
            if h == 0:
                halves[i] = small.tile([P, 2, 6], F32, name="stats")
            nc.vector.bn_stats(out=halves[i][:, h, :], in_=s_banks[i, h][:])

        def mean_and_variance(i):
            g, t = divmod(i, GROUP)
            if t == 0:
                mean_var[g] = small.tile([P, GROUP, 2], F32, name="mean_var")
            nc.vector.bn_aggr(out=mean_var[g][:, t, :], in_=halves[i][:].rearrange("p h s -> p (h s)"))

        def turn_factors(g):
            scaled_var = small.tile([P, GROUP], F32, name="scaled_var")
            nc.scalar.activation(
                out=scaled_var[:],
                in_=mean_var[g][:, :, 1],
                func=ACT.Copy,
                scale=TWO_PI * TWO_PI * ROWS / (ROWS - 1),
                bias=TWO_PI * TWO_PI * EPS,
            )
            minus_mean[g] = small.tile([P, GROUP], F32, name="minus_mean")
            nc.scalar.mul(out=minus_mean[g][:], in_=mean_var[g][:, :, 0], mul=-1.0)
            turn_scale[g] = small.tile([P, GROUP], F32, name="turn_scale")
            nc.gpsimd.tensor_tensor(out=turn_scale[g][:], in0=scaled_var[:], in1=neg_half[:], op=ALU.pow)

        def biases(g):
            turn_bias[g] = small.tile([P, GROUP], F32, name="turn_bias")
            nc.gpsimd.tensor_tensor(
                out=turn_bias[g][:], in0=minus_mean[g][:], in1=turn_scale[g][:], op=ALU.mult
            )

        def sine_factor(g):
            sine_bias[g] = small.tile([P, GROUP], F32, name="sine_bias")
            nc.scalar.mul(out=sine_bias[g][:], in_=turn_bias[g][:], mul=TWO_PI)

        def of_tile(factor, i):
            g, t = divmod(i, GROUP)
            return factor[g][:, t : t + 1]

        def copy_scores(i, h):
            if h == 0:
                raw[i] = raw_pool.tile([P, ROWS], F32, name="raw")
            nc.scalar.copy(out=raw[i][:, h * 512 : (h + 1) * 512], in_=s_banks[i, h][:])

        def shift(i):
            whole[i] = angles.tile([P, ROWS], I32, name="whole")
            engine = nc.vector if i in (3,) else nc.gpsimd
            engine.tensor_scalar(
                out=whole[i][:], in0=raw[i][:], scalar1=of_tile(turn_scale, i), scalar2=of_tile(turn_bias, i), op0=ALU.mult, op1=ALU.add
            )

        def fraction(i, h):
            if h == 0:
                unbiased[i] = angles.tile([P, ROWS], F32, name="unbiased")
            keys = slice(h * 512, (h + 1) * 512)
            nc.vector.scalar_tensor_tensor(
                out=unbiased[i][:, keys],
                in0=s_banks[i, h][:],
                scalar=of_tile(turn_scale, i),
                in1=whole[i][:, keys],
                op0=ALU.mult,
                op1=ALU.subtract,
            )

        def sine(i):
            nc.scalar.activation(
                out=sines[:, i, :], in_=unbiased[i][:], func=ACT.Sin, scale=TWO_PI, bias=of_tile(sine_bias, i)
            )

        v_banks = {}

        def v_products(b):
            g, c = divmod(b, FEATURES // P)
            feats = slice(c * P, (c + 1) * P)
            v_banks[b] = acc_banks.tile([P, PACK, P], F32, tag="acc", name="v_bank")
            for j in range(PACK):
                rows = slice((PACK * g + j) * P, (PACK * g + j + 1) * P)
                nc.tensor.matmul_mx(
                    out=v_banks[b][:, j, :],
                    lhsT=x_codes[:, rows].bitcast(FP8X4),
                    lhsT_scale=x_scales[:, rows],
                    rhs=wv_codes[:, feats].bitcast(FP8X4),
                    rhs_scale=wv_scales[:, feats],
                    start=True,
                    stop=True,
                )

        def v_add(b):
            g, c = divmod(b, FEATURES // P)
            feats = slice(c * P, (c + 1) * P)
            nc.vector.tensor_tensor(
                out=v_grouped[:, g, feats, :],
                in0=v_banks[b][:].rearrange("p j o -> p o j"),
                in1=bias_all[:, feats].unsqueeze(2).to_broadcast([P, P, PACK]),
                op=ALU.add,
            )

        def v_quantise(g):
            nc.vector.quantize_mx(
                out=v_codes[:, g, :].bitcast(FP8X4),
                scales=v_scales[:, g, :],
                in_=v_grouped[:, g, :, :].rearrange("p o j -> p (o j)"),
            )

        exp_bias, e_rows, row_sum, inv_sum, e_banks, e_grouped, e_ops, out_banks = {}, {}, {}, {}, {}, {}, {}, {}

        def row_max(i):
            top = small.tile([P, 1], F32, name="top")
            nc.vector.tensor_reduce(out=top[:], in_=sines[:, i, :], axis=AXIS.X, op=ALU.max)
            exp_bias[i] = small.tile([P, 1], F32, name="exp_bias")
            nc.gpsimd.tensor_scalar(
                out=exp_bias[i][:], in0=top[:], scalar1=-INV_SQRT_FEATURES, scalar2=0.0, op0=ALU.mult, op1=ALU.add
            )

        def exponential(i):
            e_rows[i] = e_pool.tile([P, ROWS], BF16, name="e_rows")
            pair, t = divmod(i, 2)
            if t == 0:
                row_sum[pair] = small.tile([P, 2], F32, name="row_sum")
            nc.scalar.activation(
                out=e_rows[i][:],
                in_=sines[:, i, :],
                func=ACT.Exp,
                bias=exp_bias[i][:, 0:1],
                scale=INV_SQRT_FEATURES,
                accum_out=row_sum[pair][:, t : t + 1],
            )

        def invert_sums(pair):
            inv_sum[pair] = small.tile([P, 2], F32, name="inv_sum")
            nc.vector.reciprocal(out=inv_sum[pair][:], in_=row_sum[pair][:])

        def e_quantise(i):
            codes = e_pool.tile([P, KEY_PASSES * P], U32, align_bytes=64, name="e_codes")
            scales = e_pool.tile([P, KEY_PASSES * P], U8, align_bytes=64, name="e_scales")
            nc.vector.quantize_mx(out=codes[:].bitcast(FP8X4), scales=scales[:], in_=e_grouped[i][:])
            e_ops[i] = (codes, scales)

        def e_times_v(i):
            codes, scales = e_ops[i]
            out_banks[i] = acc_banks.tile([P, FEATURES], F32, tag="acc", name="out_bank")
            for g in range(KEY_PASSES):
                queries = slice(g * P, (g + 1) * P)
                nc.tensor.matmul_mx(
                    out=out_banks[i][:],
                    lhsT=codes[:, queries].bitcast(FP8X4),
                    lhsT_scale=scales[:, queries],
                    rhs=v_codes[:, g, :].bitcast(FP8X4),
                    rhs_scale=v_scales[:, g, :],
                    start=(g == 0),
                    stop=(g == KEY_PASSES - 1),
                )

        def finish(i, on_vec):
            pair, t = divmod(i, 2)
            inverse = inv_sum[pair][:, t : t + 1]
            result = out_pool.tile([P, FEATURES], F32, name="result")
            if on_vec:
                nc.vector.tensor_scalar(
                    out=result[:], in0=out_banks[i][:], scalar1=inverse, scalar2=None, op0=ALU.mult
                )
            else:
                nc.scalar.activation(out=result[:], in_=out_banks[i][:], func=ACT.Copy, scale=inverse)
            nc.sync.dma_start(out=out[i * P : (i + 1) * P, :], in_=result[:])

        pending = []

        def fetch(name, c, copy):
            block_a, block_b, codes, scales = blocks_of(name, c)
            pending.append((group_words(copy, transpose_pair(block_a, block_b)), codes, scales, c))

        def settle():
            quantise(*pending.pop(0))


        wide = {}

        def fetch_half(name, c):
            block_a, block_b, codes, scales = blocks_of(name, c)
            if c % 2 == 0:
                wide[name] = wide_pool.tile([P, 4 * P * PACK], BF16, align_bytes=64, name="wide")
            half = slice((c % 2) * 2 * P * PACK, (c % 2 + 1) * 2 * P * PACK)
            group_words(on_scalar, transpose_pair(block_a, block_b), wide[name][:, half])
            if c % 2 == 1:
                quantise(wide[name], codes, scales, c - 1, width=4 * P)

        with tc.tile_pool(name="angles", bufs=4) as angles:
            fetch("q", 0, on_scalar)
            fetch("k", 0, on_scalar)
            settle()
            fetch("k", 1, on_scalar)
            settle()
            fetch("k", 2, on_scalar)
            settle()
            fetch("k", 3, on_scalar)
            settle()
            settle()
            for i in range(ROW_TILES):
                if i in (0, 2, 4):
                    fetch("q", i // 2 + 1, on_scalar)
                for h in range(2):
                    scores(i, h)
                    statistics(i, h)
                    copy_scores(i, h)
                mean_and_variance(i)
                if i in (0, 2, 4):
                    settle()
                if i % GROUP == GROUP - 1:
                    turn_factors(i // GROUP)
                    biases(i // GROUP)
            for i in range(ROW_TILES):
                shift(i)
                for h in range(2):
                    scores(i, h)
                    fraction(i, h)
                if i % GROUP == 0:
                    sine_factor(i // GROUP)
                sine(i)
                if i == 3:
                    row_max(0)
                if i < 6:
                    fetch_half(*(("w", i) if i < 2 else ("x", i - 2)))


        e_pool = ctx.enter_context(tc.tile_pool(name="e", bufs=4))
        for b in range(4):
            v_products(b)
        for j in range(1, 3):
            row_max(j)
        for j in range(ROW_TILES + 3 + 1):
            if j < ROW_TILES:
                exponential(j)
                e_banks[j] = transpose_pair(e_rows[j][:, 0:512], e_rows[j][:, 512:1024])
            if j + 3 < ROW_TILES:
                row_max(j + 3)
            for b in range(2 * j, min(2 * j + 2, 8)):
                v_add(b)
                if b < 4:
                    v_products(b + 4)
                if b % 4 == 3:
                    v_quantise(b // 4)
            if 1 <= j <= ROW_TILES:
                e_grouped[j - 1] = group_words(on_vector if j - 1 in (6, 7) else on_scalar, e_banks[j - 1])
                if j % 2 == 0:
                    invert_sums(j // 2 - 1)
            if 3 <= j < ROW_TILES + 3:
                e_quantise(j - 3)
                e_times_v(j - 3)
            if j >= 3 + 1:
                finish(j - 3 - 1, j - 3 - 1 in (0, 1, 2))
